import numpy as np
import ml_dtypes


def mxq(x, axis, fmt="e4m3"):
    dtype, down = {"e4m3": (ml_dtypes.float8_e4m3fn, 7), "e5m2": (ml_dtypes.float8_e5m2, 14)}[fmt]
    v = np.moveaxis(np.asarray(x, np.float32).astype(ml_dtypes.bfloat16).astype(np.float64), axis, -1)
    blocks = v.reshape(v.shape[:-1] + (-1, 32))
    amax = np.abs(blocks).max(-1, keepdims=True)
    byte = np.maximum(np.where(amax > 0, np.frexp(amax)[1] - 1 + 127, 0) - down, 1)
    scale = np.exp2(byte - 127.0)
    codes = (blocks / scale).astype(np.float32).astype(dtype).astype(np.float64)
    return np.moveaxis((codes * scale).reshape(v.shape), -1, axis)


WIDE = False


def mx_kscale(k):
    if not WIDE:
        return np.ones(k)
    levels = np.array([10, -10, 5, -5, 0])
    a = np.random.permutation(np.resize(levels, k // 512 * 4)).reshape(k // 512, 4)
    idx = np.arange(k)
    return np.exp2(a[idx // 512, idx % 128 // 32])


BF16 = ml_dtypes.bfloat16


def bf(x):
    return np.asarray(x, np.float32).astype(BF16)


def f64(x):
    return np.asarray(x).astype(np.float64)


N, C_IN, C_OUT, C_DGRAM, C_AA, C_ESM = 32, 16384, 128, 39, 22, 1280
LN_EPS = 1e-5


def layer_norm(x, g, b):
    mu = x.mean(-1, keepdims=True)
    var = x.var(-1, keepdims=True)
    return (x - mu) * (1.0 / np.sqrt(var + LN_EPS)) * g + b


def setup_inputs():
    rn, ru = np.random.standard_normal, np.random.uniform
    s = mx_kscale(C_IN)

    def vec():
        return bf(rn(C_OUT) * 0.1)

    def row():
        return bf(rn(C_OUT)[None, :])

    return {
        "act_dgram": bf(rn((N, N, C_OUT)) * 0.2),
        "aa_proj1": bf(rn((N, C_OUT)) * 0.6),
        "aa_proj2": bf(rn((N, C_OUT)) * 0.6),
        "esm_proj1": bf(rn((N, C_OUT))),
        "esm_proj2": bf(rn((N, C_OUT))),
        "query_embedding": bf(rn((N, N, C_IN)) * (0.5 + 1.5 * ru(size=(N, N)))[..., None] + rn((N, N))[..., None]),
        "pseudo_beta_mask": bf(ru(size=N)),
        "backbone_mask": bf(ru(size=N)),
        "multichain_mask_2d": bf(ru(size=(N, N))),
        "unit_x": bf(rn((N, N))),
        "unit_y": bf(rn((N, N))),
        "unit_z": bf(rn((N, N))),
        "ln_g": bf((1.0 + 0.1 * rn(C_IN)) * s),
        "ln_b": bf(0.1 * rn(C_IN) * s),
        "w_q": bf(rn((C_IN, C_OUT)) / np.sqrt(C_IN) / s[:, None]),
        "b_q": vec(),
        "w_pbm": row(), "b_pbm": vec(),
        "w_x": row(), "b_x": vec(),
        "w_y": row(), "b_y": vec(),
        "w_z": row(), "b_z": vec(),
        "w_bb": row(), "b_bb": vec(),
    }


def reference(act_dgram, aa_proj1, aa_proj2, esm_proj1, esm_proj2, query_embedding,
              pseudo_beta_mask, backbone_mask, multichain_mask_2d, unit_x, unit_y, unit_z,
              ln_g, ln_b, w_q, b_q, w_pbm, b_pbm, w_x, b_x, w_y, b_y, w_z, b_z, w_bb, b_bb):
    pbm, bbm, mc = f64(pseudo_beta_mask), f64(backbone_mask), f64(multichain_mask_2d)
    pb2 = pbm[:, None] * pbm[None, :] * mc
    bb2 = bbm[:, None] * bbm[None, :] * mc
    act = f64(act_dgram)
    act = act + (pb2[..., None] * f64(w_pbm)[0] + f64(b_pbm))
    act = act + f64(aa_proj1)[None, :, :]
    act = act + f64(aa_proj2)[:, None, :]
    act = act + ((f64(unit_x) * bb2)[..., None] * f64(w_x)[0] + f64(b_x))
    act = act + ((f64(unit_y) * bb2)[..., None] * f64(w_y)[0] + f64(b_y))
    act = act + ((f64(unit_z) * bb2)[..., None] * f64(w_z)[0] + f64(b_z))
    act = act + (bb2[..., None] * f64(w_bb)[0] + f64(b_bb))
    act = act + f64(esm_proj1)[None, :, :]
    act = act + f64(esm_proj2)[:, None, :]
    q = layer_norm(f64(query_embedding), f64(ln_g), f64(ln_b))
    act = act + (mxq(q, 2, "e4m3") @ mxq(f64(w_q), 0, "e4m3")) + f64(b_q)
    return act

@@ -1,0 +1,331 @@
+from contextlib import ExitStack
+
+import concourse.mybir as mybir
+from concourse.masks import make_identity
+
+F32 = mybir.dt.float32
+BF16 = mybir.dt.bfloat16
+U32 = mybir.dt.uint32
+U8 = mybir.dt.uint8
+FP8X4 = mybir.dt.float8_e4m3fn_x4
+ALU = mybir.AluOpType
+ACT = mybir.ActivationFunctionType
+
+P = 128
+N_RES = 32
+ROWS = N_RES * N_RES
+K = 16384
+C_OUT = 128
+LN_EPS = 1e-5
+
+PACK = 4
+K_PASS = P * PACK
+PASSES = K // K_PASS
+GROUPS = ROWS // P
+CHUNK_PASSES = 4
+CHUNK = CHUNK_PASSES * K_PASS
+CHUNKS = K // CHUNK
+CHUNK_WORDS = CHUNK // PACK
+K_BLOCKS = K // P
+
+BN_WIDTH = 512
+BN_DIM = 6
+BN_PER_CHUNK = CHUNK // BN_WIDTH
+RUN = 4
+
+FLOPS = 2 * ROWS * K * C_OUT
+
+
+def regroup_views(grouped, planes):
+    dst = grouped.rearrange("p (w i) t -> p w t i", i=RUN)
+    src = planes.rearrange("p t (w i) -> p w t i", i=RUN)
+    return dst, src
+
+
+def tile_templatepairembeddermultimer_pa_k_kernel(
+    tc,
+    act_dgram,
+    aa_proj1,
+    aa_proj2,
+    esm_proj1,
+    esm_proj2,
+    query_embedding,
+    pseudo_beta_mask,
+    backbone_mask,
+    multichain_mask_2d,
+    unit_x,
+    unit_y,
+    unit_z,
+    ln_g,
+    ln_b,
+    w_q,
+    b_q,
+    w_pbm,
+    b_pbm,
+    w_x,
+    b_x,
+    w_y,
+    b_y,
+    w_z,
+    b_z,
+    w_bb,
+    b_bb,
+    out,
+):
+    nc = tc.nc
+    x_rows = query_embedding.flatten_outer_dims()
+    out_rows = out.flatten_outer_dims()
+
+    with ExitStack() as pools:
+        const = pools.enter_context(tc.tile_pool(name="const", bufs=1))
+        w_loads = pools.enter_context(tc.tile_pool(name="w_loads", bufs=CHUNKS))
+        w_stage = pools.enter_context(tc.tile_pool(name="w_stage", bufs=2))
+        x_pool = pools.enter_context(tc.tile_pool(name="x_pool", bufs=12))
+        work = pools.enter_context(tc.tile_pool(name="work", bufs=3))
+        small = pools.enter_context(tc.tile_pool(name="small", bufs=2))
+        banks = pools.enter_context(tc.psum_pool(name="banks", bufs=6))
+        sums = pools.enter_context(tc.psum_pool(name="sums", bufs=2))
+
+        ident = const.tile([P, P], F32, name="ident")
+        make_identity(nc, ident[:])
+        eps_col = const.tile([P, 1], F32, name="eps_col")
+        nc.vector.memset(eps_col[:], LN_EPS)
+
+        def k_block_columns(vec, name):
+            rows_bf16 = const.tile([P, P], BF16, name=name + "_rows_bf16")
+            nc.sync.dma_start(out=rows_bf16[:], in_=vec.rearrange("(b p) -> b p", p=P))
+            rows_f32 = const.tile([P, P], F32, name=name + "_rows_f32")
+            nc.vector.tensor_copy(out=rows_f32[:], in_=rows_bf16[:])
+            flipped = banks.tile([P, P], F32, name=name + "_flipped", tag="bank")
+            nc.tensor.transpose(out=flipped[:], in_=rows_f32[:], identity=ident[:])
+            cols = const.tile([P, K_BLOCKS], F32, name=name + "_cols")
+            nc.vector.tensor_copy(out=cols[:], in_=flipped[:])
+            return cols
+
+        gain_cols = k_block_columns(ln_g, "gain")
+        shift_cols = k_block_columns(ln_b, "shift")
+
+        x_chunks = {}
+        stats_of = {}
+        scalars_of = {}
+
+        def load_x(n, c):
+            x_chunk = x_pool.tile([P, CHUNK], BF16, name="x_chunk")
+            nc.sync.dma_start(
+                out=x_chunk[:], in_=x_rows[n * P : (n + 1) * P, c * CHUNK : (c + 1) * CHUNK]
+            )
+            x_chunks[(n, c)] = x_chunk
+
+        def chunk_stats(n, c):
+            if c == 0:
+                stats_of[n] = small.tile([P, K // BN_WIDTH, BN_DIM], F32, name="stats")
+            for s in range(BN_PER_CHUNK):
+                nc.vector.bn_stats(
+                    out=stats_of[n][:, c * BN_PER_CHUNK + s, :],
+                    in_=x_chunks[(n, c)][:, s * BN_WIDTH : (s + 1) * BN_WIDTH],
+                )
+
+        def finish_stats(n):
+            mean_var = small.tile([P, 2], F32, name="mean_var")
+            nc.vector.bn_aggr(out=mean_var[:], in_=stats_of[n][:].rearrange("p b s -> p (b s)"))
+            mean = mean_var[:, 0:1]
+            var = mean_var[:, 1:2]
+            rough = small.tile([P, 1], F32, name="rough")
+            nc.scalar.activation(
+                out=rough[:], in_=var, func=ACT.Abs_reciprocal_sqrt, bias=eps_col[:], scale=1.0
+            )
+            var_eps = small.tile([P, 1], F32, name="var_eps")
+            nc.vector.tensor_scalar_add(out=var_eps[:], in0=var, scalar1=LN_EPS)
+            ratio = small.tile([P, 1], F32, name="ratio")
+            nc.vector.scalar_tensor_tensor(
+                out=ratio[:], in0=var_eps[:], scalar=rough[:], in1=rough[:], op0=ALU.mult, op1=ALU.mult
+            )
+            newton = small.tile([P, 1], F32, name="newton")
+            nc.vector.tensor_scalar(
+                out=newton[:], in0=ratio[:], scalar1=-0.5, scalar2=1.5, op0=ALU.mult, op1=ALU.add
+            )
+            rstd = small.tile([P, 1], F32, name="rstd")
+            nc.vector.tensor_mul(out=rstd[:], in0=rough[:], in1=newton[:])
+            offset = small.tile([P, 1], F32, name="offset")
+            nc.vector.scalar_tensor_tensor(
+                out=offset[:], in0=mean, scalar=-1.0, in1=rstd[:], op0=ALU.mult, op1=ALU.mult
+            )
+            scalars_of[n] = (mean, rstd, offset)
+
+        w_codes = const.tile([P, PASSES * C_OUT], U32, name="w_codes", align_bytes=64)
+        w_scales = const.tile([P, PASSES * C_OUT], U8, name="w_scales", align_bytes=64)
+        w_blocks = w_q.rearrange("(b p) n -> p b n", p=P)
+        w_raws = {}
+
+        def load_w(c):
+            w_raw = w_loads.tile([P, CHUNK_PASSES * PACK, C_OUT], BF16, name="w_raw")
+            first = c * CHUNK_PASSES * PACK
+            nc.sync.dma_start(out=w_raw[:], in_=w_blocks[:, first : first + CHUNK_PASSES * PACK, :])
+            w_raws[c] = w_raw
+
+        def quantise_w(c):
+            w_grouped = w_stage.tile([P, CHUNK_WORDS, PACK], BF16, name="w_grouped", align_bytes=64)
+            for a in range(CHUNK_PASSES):
+                dst, src = regroup_views(
+                    w_grouped[:, a * C_OUT : (a + 1) * C_OUT, :],
+                    w_raws[c][:, a * PACK : (a + 1) * PACK, :],
+                )
+                nc.scalar.copy(out=dst, in_=src)
+            words = slice(c * CHUNK_WORDS, (c + 1) * CHUNK_WORDS)
+            nc.vector.quantize_mx(
+                out=w_codes[:, words].bitcast(FP8X4),
+                scales=w_scales[:, words],
+                in_=w_grouped[:].rearrange("p w t -> p (w t)"),
+            )
+
+        for c in range(CHUNKS):
+            load_x(0, c)
+            load_w(c)
+        for c in range(CHUNKS):
+            chunk_stats(0, c)
+        finish_stats(0)
+        for c in range(CHUNKS):
+            quantise_w(c)
+
+        unit = const.tile([N_RES, ROWS], BF16, name="unit")
+        chain = const.tile([N_RES, ROWS], BF16, name="chain")
+        resid = const.tile([N_RES, N_RES], BF16, name="resid")
+        nc.gpsimd.memset(unit[:], 1.0)
+        nc.gpsimd.memset(chain[:], 1.0)
+        nc.gpsimd.memset(resid[:], 1.0)
+        for f, vec in enumerate((unit_x, unit_y, unit_z)):
+            nc.gpsimd.dma_start(
+                out=unit[f + 1 : f + 2, :], in_=vec.rearrange("i j -> (i j)").unsqueeze(0)
+            )
+        nc.gpsimd.dma_start(
+            out=chain[0:5, :], in_=multichain_mask_2d.rearrange("i j -> (i j)").partition_broadcast(5)
+        )
+        nc.gpsimd.dma_start(out=resid[0:1, :], in_=pseudo_beta_mask.unsqueeze(0))
+        nc.gpsimd.dma_start(out=resid[1:5, :], in_=backbone_mask.partition_broadcast(4))
+
+        features = const.tile([P, ROWS], F32, name="features")
+        pair_shape = [N_RES, N_RES, N_RES]
+        nc.gpsimd.memset(features[:], 0.0)
+        masked = features[0:N_RES, :]
+        masked_ij = masked.rearrange("f (i j) -> f i j", j=N_RES)
+        nc.gpsimd.tensor_tensor(out=masked, in0=unit[:], in1=chain[:], op=ALU.mult)
+        nc.gpsimd.tensor_tensor(
+            out=masked_ij, in0=masked_ij, in1=resid[:].unsqueeze(2).to_broadcast(pair_shape), op=ALU.mult
+        )
+        nc.gpsimd.tensor_tensor(
+            out=masked_ij, in0=masked_ij, in1=resid[:].unsqueeze(1).to_broadcast(pair_shape), op=ALU.mult
+        )
+        nc.gpsimd.tensor_copy(
+            out=features[32:64, :].rearrange("f (i j) -> f i j", j=N_RES),
+            in_=ident[32:64, 32:64].unsqueeze(1).to_broadcast(pair_shape),
+        )
+        nc.gpsimd.tensor_copy(
+            out=features[64:96, :].rearrange("f (i j) -> f i j", j=N_RES),
+            in_=ident[64:96, 64:96].unsqueeze(2).to_broadcast(pair_shape),
+        )
+
+        vectors_a = const.tile([P, C_OUT], BF16, name="vectors_a")
+        vectors_b = const.tile([P, C_OUT], BF16, name="vectors_b")
+        nc.gpsimd.memset(vectors_a[:], 0.0)
+        nc.gpsimd.memset(vectors_b[:], 0.0)
+        single_rows = (
+            w_pbm,
+            w_x,
+            w_y,
+            w_z,
+            w_bb,
+            b_q.unsqueeze(0),
+            b_pbm.unsqueeze(0),
+            b_x.unsqueeze(0),
+            b_y.unsqueeze(0),
+            b_z.unsqueeze(0),
+            b_bb.unsqueeze(0),
+        )
+        for f, vec in enumerate(single_rows):
+            nc.gpsimd.dma_start(out=vectors_a[f : f + 1, :], in_=vec)
+        nc.gpsimd.dma_start(out=vectors_a[32:64, :], in_=aa_proj1)
+        nc.gpsimd.dma_start(out=vectors_b[32:64, :], in_=esm_proj1)
+        nc.gpsimd.dma_start(out=vectors_a[64:96, :], in_=aa_proj2)
+        nc.gpsimd.dma_start(out=vectors_b[64:96, :], in_=esm_proj2)
+        feature_w = const.tile([P, C_OUT], F32, name="feature_w")
+        nc.gpsimd.tensor_tensor(out=feature_w[:], in0=vectors_a[:], in1=vectors_b[:], op=ALU.add)
+
+        dgram = const.tile([P, GROUPS, C_OUT], BF16, name="dgram")
+        nc.gpsimd.dma_start(
+            out=dgram[:], in_=act_dgram.flatten_outer_dims().rearrange("(n p) c -> p n c", p=P)
+        )
+        for n in range(GROUPS):
+            mean, rstd, offset = scalars_of[n]
+            product = sums.tile([P, C_OUT], F32, name="product")
+            for c in range(CHUNKS):
+                if n + 1 < GROUPS:
+                    load_x(n + 1, c)
+                    chunk_stats(n + 1, c)
+                    if c == CHUNKS - 1:
+                        finish_stats(n + 1)
+
+                x_hat = work.tile([P, CHUNK], F32, name="x_hat")
+                if c % 2 == 0:
+                    nc.vector.tensor_scalar(
+                        out=x_hat[:],
+                        in0=x_chunks[(n, c)][:],
+                        scalar1=mean,
+                        scalar2=rstd[:],
+                        op0=ALU.subtract,
+                        op1=ALU.mult,
+                    )
+                else:
+                    nc.scalar.activation(
+                        out=x_hat[:], in_=x_chunks[(n, c)][:], func=ACT.Identity, scale=rstd[:], bias=offset[:]
+                    )
+
+                planes = work.tile([P, PACK, CHUNK_WORDS], BF16, name="planes")
+                for a in range(CHUNK_PASSES):
+                    flipped = banks.tile([P, PACK, P], F32, name="flipped", tag="bank")
+                    for t in range(PACK):
+                        b = a * PACK + t
+                        nc.tensor.transpose(
+                            out=flipped[:, t, :], in_=x_hat[:, b * P : (b + 1) * P], identity=ident[:]
+                        )
+                    for t in range(PACK):
+                        b = (c * CHUNK_PASSES + a) * PACK + t
+                        nc.scalar.activation(
+                            out=planes[:, t, a * P : (a + 1) * P],
+                            in_=flipped[:, t, :],
+                            func=ACT.Identity,
+                            scale=gain_cols[:, b : b + 1],
+                            bias=shift_cols[:, b : b + 1],
+                        )
+
+                grouped = work.tile([P, CHUNK_WORDS, PACK], BF16, name="grouped", align_bytes=64)
+                dst, src = regroup_views(grouped[:], planes[:])
+                nc.vector.tensor_copy(out=dst, in_=src)
+                q_codes = work.tile([P, CHUNK_WORDS], U32, name="q_codes", align_bytes=64)
+                q_scales = work.tile([P, CHUNK_WORDS], U8, name="q_scales", align_bytes=64)
+                nc.vector.quantize_mx(
+                    out=q_codes[:].bitcast(FP8X4),
+                    scales=q_scales[:],
+                    in_=grouped[:].rearrange("p w t -> p (w t)"),
+                )
+
+                for a in range(CHUNK_PASSES):
+                    g = c * CHUNK_PASSES + a
+                    nc.tensor.matmul_mx(
+                        out=product[:],
+                        lhsT=q_codes[:, a * P : (a + 1) * P].bitcast(FP8X4),
+                        lhsT_scale=q_scales[:, a * P : (a + 1) * P],
+                        rhs=w_codes[:, g * C_OUT : (g + 1) * C_OUT].bitcast(FP8X4),
+                        rhs_scale=w_scales[:, g * C_OUT : (g + 1) * C_OUT],
+                        start=(g == 0),
+                        stop=(g == PASSES - 1),
+                    )
+
+            extra = banks.tile([P, C_OUT], F32, name="extra", tag="bank")
+            nc.tensor.matmul(
+                out=extra[:], lhsT=features[:, n * P : (n + 1) * P], rhs=feature_w[:], start=True, stop=True
+            )
+            others = small.tile([P, C_OUT], F32, name="others")
+            nc.vector.tensor_tensor(out=others[:], in0=extra[:], in1=dgram[:, n, :], op=ALU.add)
+            result = small.tile([P, C_OUT], F32, name="result")
+            nc.vector.tensor_tensor(out=result[:], in0=product[:], in1=others[:], op=ALU.add)
+            nc.sync.dma_start(out=out_rows[n * P : (n + 1) * P, :], in_=result[:])

@@ -32,6 +32,8 @@ BN_WIDTH = 512
 BN_DIM = 6
 BN_PER_CHUNK = CHUNK // BN_WIDTH
 RUN = 4
+STEPS = GROUPS * CHUNKS
+LOAD_AHEAD = 4
 
 FLOPS = 2 * ROWS * K * C_OUT
 
@@ -80,7 +82,7 @@ def tile_templatepairembeddermultimer_pa_k_kernel(
         const = pools.enter_context(tc.tile_pool(name="const", bufs=1))
         w_loads = pools.enter_context(tc.tile_pool(name="w_loads", bufs=CHUNKS))
         w_stage = pools.enter_context(tc.tile_pool(name="w_stage", bufs=2))
-        x_pool = pools.enter_context(tc.tile_pool(name="x_pool", bufs=12))
+        x_pool = pools.enter_context(tc.tile_pool(name="x_pool", bufs=CHUNKS + LOAD_AHEAD + 1))
         work = pools.enter_context(tc.tile_pool(name="work", bufs=3))
         small = pools.enter_context(tc.tile_pool(name="small", bufs=2))
         banks = pools.enter_context(tc.psum_pool(name="banks", bufs=6))
@@ -109,21 +111,25 @@ def tile_templatepairembeddermultimer_pa_k_kernel(
         stats_of = {}
         scalars_of = {}
 
-        def load_x(n, c):
+        def load_x(s):
+            n, c = divmod(s, CHUNKS)
             x_chunk = x_pool.tile([P, CHUNK], BF16, name="x_chunk")
             nc.sync.dma_start(
                 out=x_chunk[:], in_=x_rows[n * P : (n + 1) * P, c * CHUNK : (c + 1) * CHUNK]
             )
-            x_chunks[(n, c)] = x_chunk
+            x_chunks[s] = x_chunk
 
-        def chunk_stats(n, c):
+        def chunk_stats(s):
+            n, c = divmod(s, CHUNKS)
             if c == 0:
                 stats_of[n] = small.tile([P, K // BN_WIDTH, BN_DIM], F32, name="stats")
-            for s in range(BN_PER_CHUNK):
+            for piece in range(BN_PER_CHUNK):
                 nc.vector.bn_stats(
-                    out=stats_of[n][:, c * BN_PER_CHUNK + s, :],
-                    in_=x_chunks[(n, c)][:, s * BN_WIDTH : (s + 1) * BN_WIDTH],
+                    out=stats_of[n][:, c * BN_PER_CHUNK + piece, :],
+                    in_=x_chunks[s][:, piece * BN_WIDTH : (piece + 1) * BN_WIDTH],
                 )
+            if c == CHUNKS - 1:
+                finish_stats(n)
 
         def finish_stats(n):
             mean_var = small.tile([P, 2], F32, name="mean_var")
@@ -146,11 +152,9 @@ def tile_templatepairembeddermultimer_pa_k_kernel(
             )
             rstd = small.tile([P, 1], F32, name="rstd")
             nc.vector.tensor_mul(out=rstd[:], in0=rough[:], in1=newton[:])
-            offset = small.tile([P, 1], F32, name="offset")
-            nc.vector.scalar_tensor_tensor(
-                out=offset[:], in0=mean, scalar=-1.0, in1=rstd[:], op0=ALU.mult, op1=ALU.mult
-            )
-            scalars_of[n] = (mean, rstd, offset)
+            neg_mean = small.tile([P, 1], F32, name="neg_mean")
+            nc.vector.tensor_scalar_mul(out=neg_mean[:], in0=mean, scalar1=-1.0)
+            scalars_of[n] = (neg_mean, rstd)
 
         w_codes = const.tile([P, PASSES * C_OUT], U32, name="w_codes", align_bytes=64)
         w_scales = const.tile([P, PASSES * C_OUT], U8, name="w_scales", align_bytes=64)
@@ -177,15 +181,6 @@ def tile_templatepairembeddermultimer_pa_k_kernel(
                 scales=w_scales[:, words],
                 in_=w_grouped[:].rearrange("p w t -> p (w t)"),
             )
-
-        for c in range(CHUNKS):
-            load_x(0, c)
-            load_w(c)
-        for c in range(CHUNKS):
-            chunk_stats(0, c)
-        finish_stats(0)
-        for c in range(CHUNKS):
-            quantise_w(c)
 
         unit = const.tile([N_RES, ROWS], BF16, name="unit")
         chain = const.tile([N_RES, ROWS], BF16, name="chain")
@@ -224,6 +219,11 @@ def tile_templatepairembeddermultimer_pa_k_kernel(
             in_=ident[64:96, 64:96].unsqueeze(2).to_broadcast(pair_shape),
         )
 
+        for s in range(CHUNKS):
+            load_x(s)
+            load_w(s)
+        for s in range(CHUNKS, CHUNKS + LOAD_AHEAD):
+            load_x(s)
         vectors_a = const.tile([P, C_OUT], BF16, name="vectors_a")
         vectors_b = const.tile([P, C_OUT], BF16, name="vectors_b")
         nc.gpsimd.memset(vectors_a[:], 0.0)
@@ -242,42 +242,42 @@ def tile_templatepairembeddermultimer_pa_k_kernel(
             b_bb.unsqueeze(0),
         )
         for f, vec in enumerate(single_rows):
-            nc.gpsimd.dma_start(out=vectors_a[f : f + 1, :], in_=vec)
-        nc.gpsimd.dma_start(out=vectors_a[32:64, :], in_=aa_proj1)
-        nc.gpsimd.dma_start(out=vectors_b[32:64, :], in_=esm_proj1)
-        nc.gpsimd.dma_start(out=vectors_a[64:96, :], in_=aa_proj2)
-        nc.gpsimd.dma_start(out=vectors_b[64:96, :], in_=esm_proj2)
+            nc.sync.dma_start(out=vectors_a[f : f + 1, :], in_=vec)
+        nc.sync.dma_start(out=vectors_a[32:64, :], in_=aa_proj1)
+        nc.sync.dma_start(out=vectors_b[32:64, :], in_=esm_proj1)
+        nc.sync.dma_start(out=vectors_a[64:96, :], in_=aa_proj2)
+        nc.sync.dma_start(out=vectors_b[64:96, :], in_=esm_proj2)
         feature_w = const.tile([P, C_OUT], F32, name="feature_w")
         nc.gpsimd.tensor_tensor(out=feature_w[:], in0=vectors_a[:], in1=vectors_b[:], op=ALU.add)
 
         dgram = const.tile([P, GROUPS, C_OUT], BF16, name="dgram")
-        nc.gpsimd.dma_start(
+        nc.sync.dma_start(
             out=dgram[:], in_=act_dgram.flatten_outer_dims().rearrange("(n p) c -> p n c", p=P)
         )
+        for s in range(CHUNKS):
+            chunk_stats(s)
+        for c in range(CHUNKS):
+            quantise_w(c)
+
         for n in range(GROUPS):
-            mean, rstd, offset = scalars_of[n]
             product = sums.tile([P, C_OUT], F32, name="product")
             for c in range(CHUNKS):
-                if n + 1 < GROUPS:
-                    load_x(n + 1, c)
-                    chunk_stats(n + 1, c)
-                    if c == CHUNKS - 1:
-                        finish_stats(n + 1)
+                s = n * CHUNKS + c
+                if s + CHUNKS + LOAD_AHEAD < STEPS:
+                    load_x(s + CHUNKS + LOAD_AHEAD)
+                if s + CHUNKS < STEPS:
+                    chunk_stats(s + CHUNKS)
 
+                neg_mean, rstd = scalars_of[n]
                 x_hat = work.tile([P, CHUNK], F32, name="x_hat")
-                if c % 2 == 0:
-                    nc.vector.tensor_scalar(
-                        out=x_hat[:],
-                        in0=x_chunks[(n, c)][:],
-                        scalar1=mean,
-                        scalar2=rstd[:],
-                        op0=ALU.subtract,
-                        op1=ALU.mult,
-                    )
-                else:
-                    nc.scalar.activation(
-                        out=x_hat[:], in_=x_chunks[(n, c)][:], func=ACT.Identity, scale=rstd[:], bias=offset[:]
-                    )
+                nc.gpsimd.tensor_scalar(
+                    out=x_hat[:],
+                    in0=x_chunks[s][:],
+                    scalar1=neg_mean[:],
+                    scalar2=rstd[:],
+                    op0=ALU.add,
+                    op1=ALU.mult,
+                )
 
                 planes = work.tile([P, PACK, CHUNK_WORDS], BF16, name="planes")
                 for a in range(CHUNK_PASSES):

@@ -34,6 +34,7 @@ BN_PER_CHUNK = CHUNK // BN_WIDTH
 RUN = 4
 STEPS = GROUPS * CHUNKS
 LOAD_AHEAD = 4
+VECTOR_EVERY = 3
 
 FLOPS = 2 * ROWS * K * C_OUT
 
@@ -152,9 +153,11 @@ def tile_templatepairembeddermultimer_pa_k_kernel(
             )
             rstd = small.tile([P, 1], F32, name="rstd")
             nc.vector.tensor_mul(out=rstd[:], in0=rough[:], in1=newton[:])
-            neg_mean = small.tile([P, 1], F32, name="neg_mean")
-            nc.vector.tensor_scalar_mul(out=neg_mean[:], in0=mean, scalar1=-1.0)
-            scalars_of[n] = (neg_mean, rstd)
+            offset = small.tile([P, 1], F32, name="offset")
+            nc.vector.scalar_tensor_tensor(
+                out=offset[:], in0=mean, scalar=-1.0, in1=rstd[:], op0=ALU.mult, op1=ALU.mult
+            )
+            scalars_of[n] = (mean, rstd, offset)
 
         w_codes = const.tile([P, PASSES * C_OUT], U32, name="w_codes", align_bytes=64)
         w_scales = const.tile([P, PASSES * C_OUT], U8, name="w_scales", align_bytes=64)
@@ -200,7 +203,7 @@ def tile_templatepairembeddermultimer_pa_k_kernel(
 
         features = const.tile([P, ROWS], F32, name="features")
         pair_shape = [N_RES, N_RES, N_RES]
-        nc.gpsimd.memset(features[:], 0.0)
+        nc.vector.memset(features[:], 0.0)
         masked = features[0:N_RES, :]
         masked_ij = masked.rearrange("f (i j) -> f i j", j=N_RES)
         nc.gpsimd.tensor_tensor(out=masked, in0=unit[:], in1=chain[:], op=ALU.mult)
@@ -210,11 +213,11 @@ def tile_templatepairembeddermultimer_pa_k_kernel(
         nc.gpsimd.tensor_tensor(
             out=masked_ij, in0=masked_ij, in1=resid[:].unsqueeze(1).to_broadcast(pair_shape), op=ALU.mult
         )
-        nc.gpsimd.tensor_copy(
+        nc.vector.tensor_copy(
             out=features[32:64, :].rearrange("f (i j) -> f i j", j=N_RES),
             in_=ident[32:64, 32:64].unsqueeze(1).to_broadcast(pair_shape),
         )
-        nc.gpsimd.tensor_copy(
+        nc.vector.tensor_copy(
             out=features[64:96, :].rearrange("f (i j) -> f i j", j=N_RES),
             in_=ident[64:96, 64:96].unsqueeze(2).to_broadcast(pair_shape),
         )
@@ -242,16 +245,16 @@ def tile_templatepairembeddermultimer_pa_k_kernel(
             b_bb.unsqueeze(0),
         )
         for f, vec in enumerate(single_rows):
-            nc.sync.dma_start(out=vectors_a[f : f + 1, :], in_=vec)
-        nc.sync.dma_start(out=vectors_a[32:64, :], in_=aa_proj1)
-        nc.sync.dma_start(out=vectors_b[32:64, :], in_=esm_proj1)
-        nc.sync.dma_start(out=vectors_a[64:96, :], in_=aa_proj2)
-        nc.sync.dma_start(out=vectors_b[64:96, :], in_=esm_proj2)
+            nc.gpsimd.dma_start(out=vectors_a[f : f + 1, :], in_=vec)
+        nc.gpsimd.dma_start(out=vectors_a[32:64, :], in_=aa_proj1)
+        nc.gpsimd.dma_start(out=vectors_b[32:64, :], in_=esm_proj1)
+        nc.gpsimd.dma_start(out=vectors_a[64:96, :], in_=aa_proj2)
+        nc.gpsimd.dma_start(out=vectors_b[64:96, :], in_=esm_proj2)
         feature_w = const.tile([P, C_OUT], F32, name="feature_w")
         nc.gpsimd.tensor_tensor(out=feature_w[:], in0=vectors_a[:], in1=vectors_b[:], op=ALU.add)
 
         dgram = const.tile([P, GROUPS, C_OUT], BF16, name="dgram")
-        nc.sync.dma_start(
+        nc.gpsimd.dma_start(
             out=dgram[:], in_=act_dgram.flatten_outer_dims().rearrange("(n p) c -> p n c", p=P)
         )
         for s in range(CHUNKS):
@@ -259,67 +262,78 @@ def tile_templatepairembeddermultimer_pa_k_kernel(
         for c in range(CHUNKS):
             quantise_w(c)
 
-        for n in range(GROUPS):
-            product = sums.tile([P, C_OUT], F32, name="product")
-            for c in range(CHUNKS):
-                s = n * CHUNKS + c
-                if s + CHUNKS + LOAD_AHEAD < STEPS:
-                    load_x(s + CHUNKS + LOAD_AHEAD)
-                if s + CHUNKS < STEPS:
-                    chunk_stats(s + CHUNKS)
+        grouped_of = {}
+        product_of = {}
 
-                neg_mean, rstd = scalars_of[n]
-                x_hat = work.tile([P, CHUNK], F32, name="x_hat")
-                nc.gpsimd.tensor_scalar(
+        def normalise(s):
+            mean, rstd, offset = scalars_of[s // CHUNKS]
+            x_hat = work.tile([P, CHUNK], F32, name="x_hat")
+            if s % VECTOR_EVERY == 0 or s + CHUNKS >= STEPS:
+                nc.vector.tensor_scalar(
                     out=x_hat[:],
                     in0=x_chunks[s][:],
-                    scalar1=neg_mean[:],
+                    scalar1=mean,
                     scalar2=rstd[:],
-                    op0=ALU.add,
+                    op0=ALU.subtract,
                     op1=ALU.mult,
                 )
+            else:
+                nc.scalar.activation(
+                    out=x_hat[:], in_=x_chunks[s][:], func=ACT.Identity, scale=rstd[:], bias=offset[:]
+                )
+            return x_hat
 
-                planes = work.tile([P, PACK, CHUNK_WORDS], BF16, name="planes")
-                for a in range(CHUNK_PASSES):
-                    flipped = banks.tile([P, PACK, P], F32, name="flipped", tag="bank")
-                    for t in range(PACK):
-                        b = a * PACK + t
-                        nc.tensor.transpose(
-                            out=flipped[:, t, :], in_=x_hat[:, b * P : (b + 1) * P], identity=ident[:]
-                        )
-                    for t in range(PACK):
-                        b = (c * CHUNK_PASSES + a) * PACK + t
-                        nc.scalar.activation(
-                            out=planes[:, t, a * P : (a + 1) * P],
-                            in_=flipped[:, t, :],
-                            func=ACT.Identity,
-                            scale=gain_cols[:, b : b + 1],
-                            bias=shift_cols[:, b : b + 1],
-                        )
+        def flip_scale_shift(s, x_hat):
+            c = s % CHUNKS
+            planes = work.tile([P, PACK, CHUNK_WORDS], BF16, name="planes")
+            for a in range(CHUNK_PASSES):
+                flipped = banks.tile([P, PACK, P], F32, name="flipped", tag="bank")
+                for t in range(PACK):
+                    b = a * PACK + t
+                    nc.tensor.transpose(
+                        out=flipped[:, t, :], in_=x_hat[:, b * P : (b + 1) * P], identity=ident[:]
+                    )
+                for t in range(PACK):
+                    b = (c * CHUNK_PASSES + a) * PACK + t
+                    nc.scalar.activation(
+                        out=planes[:, t, a * P : (a + 1) * P],
+                        in_=flipped[:, t, :],
+                        func=ACT.Identity,
+                        scale=gain_cols[:, b : b + 1],
+                        bias=shift_cols[:, b : b + 1],
+                    )
+            return planes
 
-                grouped = work.tile([P, CHUNK_WORDS, PACK], BF16, name="grouped", align_bytes=64)
-                dst, src = regroup_views(grouped[:], planes[:])
-                nc.vector.tensor_copy(out=dst, in_=src)
-                q_codes = work.tile([P, CHUNK_WORDS], U32, name="q_codes", align_bytes=64)
-                q_scales = work.tile([P, CHUNK_WORDS], U8, name="q_scales", align_bytes=64)
-                nc.vector.quantize_mx(
-                    out=q_codes[:].bitcast(FP8X4),
-                    scales=q_scales[:],
-                    in_=grouped[:].rearrange("p w t -> p (w t)"),
+        def regroup(s, planes):
+            grouped = work.tile([P, CHUNK_WORDS, PACK], BF16, name="grouped", align_bytes=64)
+            dst, src = regroup_views(grouped[:], planes[:])
+            nc.vector.tensor_copy(out=dst, in_=src)
+            grouped_of[s] = grouped
+
+        def quantise_multiply(s):
+            n, c = divmod(s, CHUNKS)
+            q_codes = work.tile([P, CHUNK_WORDS], U32, name="q_codes", align_bytes=64)
+            q_scales = work.tile([P, CHUNK_WORDS], U8, name="q_scales", align_bytes=64)
+            nc.vector.quantize_mx(
+                out=q_codes[:].bitcast(FP8X4),
+                scales=q_scales[:],
+                in_=grouped_of[s][:].rearrange("p w t -> p (w t)"),
+            )
+            if c == 0:
+                product_of[n] = sums.tile([P, C_OUT], F32, name="product")
+            for a in range(CHUNK_PASSES):
+                g = c * CHUNK_PASSES + a
+                nc.tensor.matmul_mx(
+                    out=product_of[n][:],
+                    lhsT=q_codes[:, a * P : (a + 1) * P].bitcast(FP8X4),
+                    lhsT_scale=q_scales[:, a * P : (a + 1) * P],
+                    rhs=w_codes[:, g * C_OUT : (g + 1) * C_OUT].bitcast(FP8X4),
+                    rhs_scale=w_scales[:, g * C_OUT : (g + 1) * C_OUT],
+                    start=(g == 0),
+                    stop=(g == PASSES - 1),
                 )
 
-                for a in range(CHUNK_PASSES):
-                    g = c * CHUNK_PASSES + a
-                    nc.tensor.matmul_mx(
-                        out=product[:],
-                        lhsT=q_codes[:, a * P : (a + 1) * P].bitcast(FP8X4),
-                        lhsT_scale=q_scales[:, a * P : (a + 1) * P],
-                        rhs=w_codes[:, g * C_OUT : (g + 1) * C_OUT].bitcast(FP8X4),
-                        rhs_scale=w_scales[:, g * C_OUT : (g + 1) * C_OUT],
-                        start=(g == 0),
-                        stop=(g == PASSES - 1),
-                    )
-
+        def store_group(n):
             extra = banks.tile([P, C_OUT], F32, name="extra", tag="bank")
             nc.tensor.matmul(
                 out=extra[:], lhsT=features[:, n * P : (n + 1) * P], rhs=feature_w[:], start=True, stop=True
@@ -327,5 +341,17 @@ def tile_templatepairembeddermultimer_pa_k_kernel(
             others = small.tile([P, C_OUT], F32, name="others")
             nc.vector.tensor_tensor(out=others[:], in0=extra[:], in1=dgram[:, n, :], op=ALU.add)
             result = small.tile([P, C_OUT], F32, name="result")
-            nc.vector.tensor_tensor(out=result[:], in0=product[:], in1=others[:], op=ALU.add)
+            nc.vector.tensor_tensor(out=result[:], in0=product_of[n][:], in1=others[:], op=ALU.add)
             nc.sync.dma_start(out=out_rows[n * P : (n + 1) * P, :], in_=result[:])
+
+        for s in range(STEPS + 1):
+            if s + CHUNKS + LOAD_AHEAD < STEPS:
+                load_x(s + CHUNKS + LOAD_AHEAD)
+            if s + CHUNKS < STEPS:
+                chunk_stats(s + CHUNKS)
+            if s < STEPS:
+                regroup(s, flip_scale_shift(s, normalise(s)))
+            if s >= 1:
+                quantise_multiply(s - 1)
+                if s % CHUNKS == 0:
+                    store_group(s // CHUNKS - 1)

@@ -34,7 +34,7 @@ BN_PER_CHUNK = CHUNK // BN_WIDTH
 RUN = 4
 STEPS = GROUPS * CHUNKS
 LOAD_AHEAD = 4
-VECTOR_EVERY = 3
+VECTOR_EVERY = 6
 
 FLOPS = 2 * ROWS * K * C_OUT
 

@@ -26,6 +26,7 @@ CHUNK_PASSES = 4
 CHUNK = CHUNK_PASSES * K_PASS
 CHUNKS = K // CHUNK
 CHUNK_WORDS = CHUNK // PACK
+CHUNK_BLOCKS = CHUNK // P
 K_BLOCKS = K // P
 
 BN_WIDTH = 512
@@ -33,8 +34,11 @@ BN_DIM = 6
 BN_PER_CHUNK = CHUNK // BN_WIDTH
 RUN = 4
 STEPS = GROUPS * CHUNKS
+STATS_LEAD = 10
 LOAD_AHEAD = 4
-VECTOR_EVERY = 6
+W_EARLY = 6
+VECTOR_BLOCKS_MAIN = 0
+VECTOR_BLOCKS_TAIL = 12
 
 FLOPS = 2 * ROWS * K * C_OUT
 
@@ -79,38 +83,33 @@ def tile_templatepairembeddermultimer_pa_k_kernel(
     x_rows = query_embedding.flatten_outer_dims()
     out_rows = out.flatten_outer_dims()
 
+
     with ExitStack() as pools:
         const = pools.enter_context(tc.tile_pool(name="const", bufs=1))
         w_loads = pools.enter_context(tc.tile_pool(name="w_loads", bufs=CHUNKS))
-        w_stage = pools.enter_context(tc.tile_pool(name="w_stage", bufs=2))
-        x_pool = pools.enter_context(tc.tile_pool(name="x_pool", bufs=CHUNKS + LOAD_AHEAD + 1))
+        w_stage = pools.enter_context(tc.tile_pool(name="w_stage", bufs=CHUNKS))
+        x_pool = pools.enter_context(tc.tile_pool(name="x_pool", bufs=STATS_LEAD + LOAD_AHEAD + 2))
         work = pools.enter_context(tc.tile_pool(name="work", bufs=3))
         small = pools.enter_context(tc.tile_pool(name="small", bufs=2))
         banks = pools.enter_context(tc.psum_pool(name="banks", bufs=6))
         sums = pools.enter_context(tc.psum_pool(name="sums", bufs=2))
+        pools.enter_context(tc.manual_schedule())
 
         ident = const.tile([P, P], F32, name="ident")
         make_identity(nc, ident[:])
         eps_col = const.tile([P, 1], F32, name="eps_col")
         nc.vector.memset(eps_col[:], LN_EPS)
+        warm = const.tile([P, 1], F32, name="warm")
+        nc.scalar.activation(out=warm[:], in_=eps_col[:], func=ACT.Abs_reciprocal_sqrt)
 
-        def k_block_columns(vec, name):
-            rows_bf16 = const.tile([P, P], BF16, name=name + "_rows_bf16")
-            nc.sync.dma_start(out=rows_bf16[:], in_=vec.rearrange("(b p) -> b p", p=P))
-            rows_f32 = const.tile([P, P], F32, name=name + "_rows_f32")
-            nc.vector.tensor_copy(out=rows_f32[:], in_=rows_bf16[:])
-            flipped = banks.tile([P, P], F32, name=name + "_flipped", tag="bank")
-            nc.tensor.transpose(out=flipped[:], in_=rows_f32[:], identity=ident[:])
-            cols = const.tile([P, K_BLOCKS], F32, name=name + "_cols")
-            nc.vector.tensor_copy(out=cols[:], in_=flipped[:])
-            return cols
-
-        gain_cols = k_block_columns(ln_g, "gain")
-        shift_cols = k_block_columns(ln_b, "shift")
+        gain_rows = const.tile([P, P], BF16, name="gain_rows")
+        shift_rows = const.tile([P, P], BF16, name="shift_rows")
+        nc.sync.dma_start(out=gain_rows[:], in_=ln_g.rearrange("(b p) -> b p", p=P))
+        nc.sync.dma_start(out=shift_rows[:], in_=ln_b.rearrange("(b p) -> b p", p=P))
 
         x_chunks = {}
-        stats_of = {}
-        scalars_of = {}
+        w_raws = {}
+        w_blocks = w_q.rearrange("(b p) n -> p b n", p=P)
 
         def load_x(s):
             n, c = divmod(s, CHUNKS)
@@ -120,77 +119,39 @@ def tile_templatepairembeddermultimer_pa_k_kernel(
             )
             x_chunks[s] = x_chunk
 
-        def chunk_stats(s):
-            n, c = divmod(s, CHUNKS)
-            if c == 0:
-                stats_of[n] = small.tile([P, K // BN_WIDTH, BN_DIM], F32, name="stats")
-            for piece in range(BN_PER_CHUNK):
-                nc.vector.bn_stats(
-                    out=stats_of[n][:, c * BN_PER_CHUNK + piece, :],
-                    in_=x_chunks[s][:, piece * BN_WIDTH : (piece + 1) * BN_WIDTH],
-                )
-            if c == CHUNKS - 1:
-                finish_stats(n)
-
-        def finish_stats(n):
-            mean_var = small.tile([P, 2], F32, name="mean_var")
-            nc.vector.bn_aggr(out=mean_var[:], in_=stats_of[n][:].rearrange("p b s -> p (b s)"))
-            mean = mean_var[:, 0:1]
-            var = mean_var[:, 1:2]
-            rough = small.tile([P, 1], F32, name="rough")
-            nc.scalar.activation(
-                out=rough[:], in_=var, func=ACT.Abs_reciprocal_sqrt, bias=eps_col[:], scale=1.0
-            )
-            var_eps = small.tile([P, 1], F32, name="var_eps")
-            nc.vector.tensor_scalar_add(out=var_eps[:], in0=var, scalar1=LN_EPS)
-            ratio = small.tile([P, 1], F32, name="ratio")
-            nc.vector.scalar_tensor_tensor(
-                out=ratio[:], in0=var_eps[:], scalar=rough[:], in1=rough[:], op0=ALU.mult, op1=ALU.mult
-            )
-            newton = small.tile([P, 1], F32, name="newton")
-            nc.vector.tensor_scalar(
-                out=newton[:], in0=ratio[:], scalar1=-0.5, scalar2=1.5, op0=ALU.mult, op1=ALU.add
-            )
-            rstd = small.tile([P, 1], F32, name="rstd")
-            nc.vector.tensor_mul(out=rstd[:], in0=rough[:], in1=newton[:])
-            offset = small.tile([P, 1], F32, name="offset")
-            nc.vector.scalar_tensor_tensor(
-                out=offset[:], in0=mean, scalar=-1.0, in1=rstd[:], op0=ALU.mult, op1=ALU.mult
-            )
-            scalars_of[n] = (mean, rstd, offset)
-
-        w_codes = const.tile([P, PASSES * C_OUT], U32, name="w_codes", align_bytes=64)
-        w_scales = const.tile([P, PASSES * C_OUT], U8, name="w_scales", align_bytes=64)
-        w_blocks = w_q.rearrange("(b p) n -> p b n", p=P)
-        w_raws = {}
-
         def load_w(c):
             w_raw = w_loads.tile([P, CHUNK_PASSES * PACK, C_OUT], BF16, name="w_raw")
             first = c * CHUNK_PASSES * PACK
             nc.sync.dma_start(out=w_raw[:], in_=w_blocks[:, first : first + CHUNK_PASSES * PACK, :])
             w_raws[c] = w_raw
 
-        def quantise_w(c):
-            w_grouped = w_stage.tile([P, CHUNK_WORDS, PACK], BF16, name="w_grouped", align_bytes=64)
-            for a in range(CHUNK_PASSES):
-                dst, src = regroup_views(
-                    w_grouped[:, a * C_OUT : (a + 1) * C_OUT, :],
-                    w_raws[c][:, a * PACK : (a + 1) * PACK, :],
-                )
-                nc.scalar.copy(out=dst, in_=src)
-            words = slice(c * CHUNK_WORDS, (c + 1) * CHUNK_WORDS)
-            nc.vector.quantize_mx(
-                out=w_codes[:, words].bitcast(FP8X4),
-                scales=w_scales[:, words],
-                in_=w_grouped[:].rearrange("p w t -> p (w t)"),
+        x_chunks[0] = x_pool.tile([P, CHUNK], BF16, name="x_chunk")
+        w_raws[0] = w_loads.tile([P, CHUNK_PASSES * PACK, C_OUT], BF16, name="w_raw")
+        for a in range(CHUNK_PASSES):
+            nc.sync.dma_start(
+                out=x_chunks[0][:, a * K_PASS : (a + 1) * K_PASS], in_=x_rows[0:P, a * K_PASS : (a + 1) * K_PASS]
             )
+            nc.sync.dma_start(
+                out=w_raws[0][:, a * PACK : (a + 1) * PACK, :], in_=w_blocks[:, a * PACK : (a + 1) * PACK, :]
+            )
+        for s in range(1, CHUNKS):
+            load_x(s)
+            load_w(s)
+        for s in range(CHUNKS, STATS_LEAD + LOAD_AHEAD - 1):
+            load_x(s)
 
         unit = const.tile([N_RES, ROWS], BF16, name="unit")
         chain = const.tile([N_RES, ROWS], BF16, name="chain")
         resid = const.tile([N_RES, N_RES], BF16, name="resid")
+        vectors_a = const.tile([P, C_OUT], BF16, name="vectors_a")
+        vectors_b = const.tile([P, C_OUT], BF16, name="vectors_b")
+        features = const.tile([P, ROWS], F32, name="features")
+        dgram = const.tile([P, GROUPS, C_OUT], BF16, name="dgram")
         nc.gpsimd.memset(unit[:], 1.0)
         nc.gpsimd.memset(chain[:], 1.0)
         nc.gpsimd.memset(resid[:], 1.0)
+        nc.gpsimd.memset(vectors_a[:], 0.0)
+        nc.gpsimd.memset(vectors_b[:], 0.0)
         for f, vec in enumerate((unit_x, unit_y, unit_z)):
             nc.gpsimd.dma_start(
                 out=unit[f + 1 : f + 2, :], in_=vec.rearrange("i j -> (i j)").unsqueeze(0)
@@ -200,37 +161,6 @@ def tile_templatepairembeddermultimer_pa_k_kernel(
         )
         nc.gpsimd.dma_start(out=resid[0:1, :], in_=pseudo_beta_mask.unsqueeze(0))
         nc.gpsimd.dma_start(out=resid[1:5, :], in_=backbone_mask.partition_broadcast(4))
-
-        features = const.tile([P, ROWS], F32, name="features")
-        pair_shape = [N_RES, N_RES, N_RES]
-        nc.vector.memset(features[:], 0.0)
-        masked = features[0:N_RES, :]
-        masked_ij = masked.rearrange("f (i j) -> f i j", j=N_RES)
-        nc.gpsimd.tensor_tensor(out=masked, in0=unit[:], in1=chain[:], op=ALU.mult)
-        nc.gpsimd.tensor_tensor(
-            out=masked_ij, in0=masked_ij, in1=resid[:].unsqueeze(2).to_broadcast(pair_shape), op=ALU.mult
-        )
-        nc.gpsimd.tensor_tensor(
-            out=masked_ij, in0=masked_ij, in1=resid[:].unsqueeze(1).to_broadcast(pair_shape), op=ALU.mult
-        )
-        nc.vector.tensor_copy(
-            out=features[32:64, :].rearrange("f (i j) -> f i j", j=N_RES),
-            in_=ident[32:64, 32:64].unsqueeze(1).to_broadcast(pair_shape),
-        )
-        nc.vector.tensor_copy(
-            out=features[64:96, :].rearrange("f (i j) -> f i j", j=N_RES),
-            in_=ident[64:96, 64:96].unsqueeze(2).to_broadcast(pair_shape),
-        )
-
-        for s in range(CHUNKS):
-            load_x(s)
-            load_w(s)
-        for s in range(CHUNKS, CHUNKS + LOAD_AHEAD):
-            load_x(s)
-        vectors_a = const.tile([P, C_OUT], BF16, name="vectors_a")
-        vectors_b = const.tile([P, C_OUT], BF16, name="vectors_b")
-        nc.gpsimd.memset(vectors_a[:], 0.0)
-        nc.gpsimd.memset(vectors_b[:], 0.0)
         single_rows = (
             w_pbm,
             w_x,
@@ -250,68 +180,184 @@ def tile_templatepairembeddermultimer_pa_k_kernel(
         nc.gpsimd.dma_start(out=vectors_b[32:64, :], in_=esm_proj1)
         nc.gpsimd.dma_start(out=vectors_a[64:96, :], in_=aa_proj2)
         nc.gpsimd.dma_start(out=vectors_b[64:96, :], in_=esm_proj2)
-        feature_w = const.tile([P, C_OUT], F32, name="feature_w")
-        nc.gpsimd.tensor_tensor(out=feature_w[:], in0=vectors_a[:], in1=vectors_b[:], op=ALU.add)
-
-        dgram = const.tile([P, GROUPS, C_OUT], BF16, name="dgram")
         nc.gpsimd.dma_start(
             out=dgram[:], in_=act_dgram.flatten_outer_dims().rearrange("(n p) c -> p n c", p=P)
         )
-        for s in range(CHUNKS):
-            chunk_stats(s)
-        for c in range(CHUNKS):
-            quantise_w(c)
+        pair_shape = [N_RES, N_RES, N_RES]
+        nc.gpsimd.memset(features[:], 0.0)
+        masked = features[0:N_RES, :]
+        masked_ij = masked.rearrange("f (i j) -> f i j", j=N_RES)
+        nc.gpsimd.tensor_tensor(out=masked, in0=unit[:], in1=chain[:], op=ALU.mult)
+        nc.gpsimd.tensor_tensor(
+            out=masked_ij, in0=masked_ij, in1=resid[:].unsqueeze(2).to_broadcast(pair_shape), op=ALU.mult
+        )
+        nc.gpsimd.tensor_tensor(
+            out=masked_ij, in0=masked_ij, in1=resid[:].unsqueeze(1).to_broadcast(pair_shape), op=ALU.mult
+        )
+        feature_w = const.tile([P, C_OUT], F32, name="feature_w")
+        nc.gpsimd.tensor_tensor(out=feature_w[:], in0=vectors_a[:], in1=vectors_b[:], op=ALU.add)
 
+        nc.gpsimd.tensor_copy(
+            out=features[32:64, :].rearrange("f (i j) -> f i j", j=N_RES),
+            in_=ident[32:64, 32:64].unsqueeze(1).to_broadcast(pair_shape),
+        )
+        nc.gpsimd.tensor_copy(
+            out=features[64:96, :].rearrange("f (i j) -> f i j", j=N_RES),
+            in_=ident[64:96, 64:96].unsqueeze(2).to_broadcast(pair_shape),
+        )
+
+        def k_block_columns(rows_bf16, name):
+            rows_f32 = const.tile([P, P], F32, name=name + "_rows_f32")
+            nc.vector.tensor_copy(out=rows_f32[:], in_=rows_bf16[:])
+            flipped = banks.tile([P, P], F32, name=name + "_flipped", tag="bank")
+            nc.tensor.transpose(out=flipped[:], in_=rows_f32[:], identity=ident[:])
+            cols = const.tile([P, K_BLOCKS], F32, name=name + "_cols")
+            nc.vector.tensor_copy(out=cols[:], in_=flipped[:])
+            return cols
+
+        gain_cols = k_block_columns(gain_rows, "gain")
+        shift_cols = k_block_columns(shift_rows, "shift")
+
+        w_codes = const.tile([P, PASSES * C_OUT], U32, name="w_codes", align_bytes=64)
+        w_scales = const.tile([P, PASSES * C_OUT], U8, name="w_scales", align_bytes=64)
+        w_grouped_of = {}
+
+        def regroup_w(c):
+            w_grouped = w_stage.tile([P, CHUNK_WORDS, PACK], BF16, name="w_grouped", align_bytes=64)
+            for a in range(CHUNK_PASSES):
+                dst, src = regroup_views(
+                    w_grouped[:, a * C_OUT : (a + 1) * C_OUT, :],
+                    w_raws[c][:, a * PACK : (a + 1) * PACK, :],
+                )
+                nc.scalar.copy(out=dst, in_=src)
+            w_grouped_of[c] = w_grouped
+
+        def quantise_w(c):
+            words = slice(c * CHUNK_WORDS, (c + 1) * CHUNK_WORDS)
+            nc.vector.quantize_mx(
+                out=w_codes[:, words].bitcast(FP8X4),
+                scales=w_scales[:, words],
+                in_=w_grouped_of[c][:].rearrange("p w t -> p (w t)"),
+            )
+
+        stats_of = {}
+        mean_var_of = {}
+        rough_of = {}
+        var_eps_of = {}
+        scalars_of = {}
+
+        def chunk_stats(s, pieces):
+            n, c = divmod(s, CHUNKS)
+            if c == 0 and pieces[0] == 0:
+                stats_of[n] = small.tile([P, K // BN_WIDTH, BN_DIM], F32, name="stats")
+            for piece in pieces:
+                nc.vector.bn_stats(
+                    out=stats_of[n][:, c * BN_PER_CHUNK + piece, :],
+                    in_=x_chunks[s][:, piece * BN_WIDTH : (piece + 1) * BN_WIDTH],
+                )
+
+        def stats_aggregate(n):
+            mean_var = small.tile([P, 2], F32, name="mean_var")
+            nc.vector.bn_aggr(out=mean_var[:], in_=stats_of[n][:].rearrange("p b s -> p (b s)"))
+            var_eps = small.tile([P, 1], F32, name="var_eps")
+            nc.vector.tensor_scalar_add(out=var_eps[:], in0=mean_var[:, 1:2], scalar1=LN_EPS)
+            mean_var_of[n] = mean_var
+            var_eps_of[n] = var_eps
+
+        def stats_table(n):
+            rough = small.tile([P, 1], F32, name="rough")
+            nc.scalar.activation(
+                out=rough[:],
+                in_=mean_var_of[n][:, 1:2],
+                func=ACT.Abs_reciprocal_sqrt,
+                bias=eps_col[:],
+                scale=1.0,
+            )
+            rough_of[n] = rough
+
+        def stats_newton(n):
+            rough = rough_of[n]
+            ratio = small.tile([P, 1], F32, name="ratio")
+            nc.vector.scalar_tensor_tensor(
+                out=ratio[:], in0=var_eps_of[n][:], scalar=rough[:], in1=rough[:], op0=ALU.mult, op1=ALU.mult
+            )
+            newton = small.tile([P, 1], F32, name="newton")
+            nc.vector.tensor_scalar(
+                out=newton[:], in0=ratio[:], scalar1=-0.5, scalar2=1.5, op0=ALU.mult, op1=ALU.add
+            )
+            rstd = small.tile([P, 1], F32, name="rstd")
+            nc.vector.tensor_mul(out=rstd[:], in0=rough[:], in1=newton[:])
+            offset = small.tile([P, 1], F32, name="offset")
+            nc.vector.scalar_tensor_tensor(
+                out=offset[:], in0=mean_var_of[n][:, 0:1], scalar=-1.0, in1=rstd[:], op0=ALU.mult, op1=ALU.mult
+            )
+            scalars_of[n] = (mean_var_of[n][:, 0:1], rstd, offset)
+
+        x_hat_of = {}
+        banks_of = {}
+        planes_of = {}
         grouped_of = {}
+        codes_of = {}
         product_of = {}
+        others_of = {}
 
         def normalise(s):
             mean, rstd, offset = scalars_of[s // CHUNKS]
             x_hat = work.tile([P, CHUNK], F32, name="x_hat")
-            if s % VECTOR_EVERY == 0 or s + CHUNKS >= STEPS:
+            has_stats = s - 1 + STATS_LEAD < STEPS
+            split = CHUNK - P * (VECTOR_BLOCKS_MAIN if has_stats else VECTOR_BLOCKS_TAIL)
+            if split > 0:
+                nc.scalar.activation(
+                    out=x_hat[:, 0:split],
+                    in_=x_chunks[s][:, 0:split],
+                    func=ACT.Identity,
+                    scale=rstd[:],
+                    bias=offset[:],
+                )
+            if split < CHUNK:
                 nc.vector.tensor_scalar(
-                    out=x_hat[:],
-                    in0=x_chunks[s][:],
+                    out=x_hat[:, split:CHUNK],
+                    in0=x_chunks[s][:, split:CHUNK],
                     scalar1=mean,
                     scalar2=rstd[:],
                     op0=ALU.subtract,
                     op1=ALU.mult,
                 )
-            else:
-                nc.scalar.activation(
-                    out=x_hat[:], in_=x_chunks[s][:], func=ACT.Identity, scale=rstd[:], bias=offset[:]
-                )
-            return x_hat
+            x_hat_of[s] = x_hat
 
-        def flip_scale_shift(s, x_hat):
-            c = s % CHUNKS
-            planes = work.tile([P, PACK, CHUNK_WORDS], BF16, name="planes")
+        def flip(s):
+            banks_of[s] = []
             for a in range(CHUNK_PASSES):
                 flipped = banks.tile([P, PACK, P], F32, name="flipped", tag="bank")
                 for t in range(PACK):
                     b = a * PACK + t
                     nc.tensor.transpose(
-                        out=flipped[:, t, :], in_=x_hat[:, b * P : (b + 1) * P], identity=ident[:]
+                        out=flipped[:, t, :], in_=x_hat_of[s][:, b * P : (b + 1) * P], identity=ident[:]
                     )
+                banks_of[s].append(flipped)
+
+        def scale_shift(s):
+            c = s % CHUNKS
+            planes = work.tile([P, PACK, CHUNK_WORDS], BF16, name="planes")
+            for a in range(CHUNK_PASSES):
                 for t in range(PACK):
                     b = (c * CHUNK_PASSES + a) * PACK + t
                     nc.scalar.activation(
                         out=planes[:, t, a * P : (a + 1) * P],
-                        in_=flipped[:, t, :],
+                        in_=banks_of[s][a][:, t, :],
                         func=ACT.Identity,
                         scale=gain_cols[:, b : b + 1],
                         bias=shift_cols[:, b : b + 1],
                     )
-            return planes
+            planes_of[s] = planes
 
-        def regroup(s, planes):
+        def regroup(s):
             grouped = work.tile([P, CHUNK_WORDS, PACK], BF16, name="grouped", align_bytes=64)
-            dst, src = regroup_views(grouped[:], planes[:])
+            dst, src = regroup_views(grouped[:], planes_of[s][:])
             nc.vector.tensor_copy(out=dst, in_=src)
             grouped_of[s] = grouped
 
-        def quantise_multiply(s):
-            n, c = divmod(s, CHUNKS)
+        def quantise(s):
             q_codes = work.tile([P, CHUNK_WORDS], U32, name="q_codes", align_bytes=64)
             q_scales = work.tile([P, CHUNK_WORDS], U8, name="q_scales", align_bytes=64)
             nc.vector.quantize_mx(
@@ -319,6 +365,11 @@ def tile_templatepairembeddermultimer_pa_k_kernel(
                 scales=q_scales[:],
                 in_=grouped_of[s][:].rearrange("p w t -> p (w t)"),
             )
+            codes_of[s] = (q_codes, q_scales)
+
+        def multiply(s):
+            n, c = divmod(s, CHUNKS)
+            q_codes, q_scales = codes_of[s]
             if c == 0:
                 product_of[n] = sums.tile([P, C_OUT], F32, name="product")
             for a in range(CHUNK_PASSES):
@@ -333,25 +384,70 @@ def tile_templatepairembeddermultimer_pa_k_kernel(
                     stop=(g == PASSES - 1),
                 )
 
-        def store_group(n):
+        def other_terms_matmul(n):
             extra = banks.tile([P, C_OUT], F32, name="extra", tag="bank")
             nc.tensor.matmul(
                 out=extra[:], lhsT=features[:, n * P : (n + 1) * P], rhs=feature_w[:], start=True, stop=True
             )
+            others_of[n] = extra
+
+        def other_terms_add(n):
             others = small.tile([P, C_OUT], F32, name="others")
-            nc.vector.tensor_tensor(out=others[:], in0=extra[:], in1=dgram[:, n, :], op=ALU.add)
+            nc.vector.tensor_tensor(out=others[:], in0=others_of[n][:], in1=dgram[:, n, :], op=ALU.add)
+            others_of[n] = others
+
+        def store_group(n):
             result = small.tile([P, C_OUT], F32, name="result")
-            nc.vector.tensor_tensor(out=result[:], in0=product_of[n][:], in1=others[:], op=ALU.add)
+            nc.vector.tensor_tensor(out=result[:], in0=product_of[n][:], in1=others_of[n][:], op=ALU.add)
             nc.sync.dma_start(out=out_rows[n * P : (n + 1) * P, :], in_=result[:])
 
-        for s in range(STEPS + 1):
-            if s + CHUNKS + LOAD_AHEAD < STEPS:
-                load_x(s + CHUNKS + LOAD_AHEAD)
-            if s + CHUNKS < STEPS:
-                chunk_stats(s + CHUNKS)
-            if s < STEPS:
-                regroup(s, flip_scale_shift(s, normalise(s)))
-            if s >= 1:
-                quantise_multiply(s - 1)
-                if s % CHUNKS == 0:
-                    store_group(s // CHUNKS - 1)
+        for c in range(W_EARLY):
+            regroup_w(c)
+        for s in range(CHUNKS):
+            chunk_stats(s, (0, 1, 2, 3))
+        stats_aggregate(0)
+        stats_table(0)
+        stats_newton(0)
+
+        first_half = (0, 1)
+        second_half = (2, 3)
+        for s in range(-1, STEPS + 4):
+            ahead = s + STATS_LEAD + LOAD_AHEAD
+            if ahead < STEPS:
+                load_x(ahead)
+            stat_chunks = tuple(range(CHUNKS, STATS_LEAD)) if s == -1 else (s + STATS_LEAD,)
+            if stat_chunks[0] >= STEPS:
+                stat_chunks = ()
+            if 0 <= s + 1 < STEPS:
+                normalise(s + 1)
+            if 0 <= s < STEPS:
+                flip(s)
+                if s % CHUNKS == 4:
+                    other_terms_matmul(s // CHUNKS)
+            if 0 <= s - 1 < STEPS:
+                regroup(s - 1)
+            for cs in stat_chunks:
+                chunk_stats(cs, first_half)
+            done = s - 1 + STATS_LEAD
+            if done < STEPS and done % CHUNKS == CHUNKS - 1 and s >= 0:
+                stats_table(done // CHUNKS)
+            if 0 <= s < STEPS:
+                scale_shift(s)
+            if 0 <= s < CHUNKS - W_EARLY:
+                regroup_w(W_EARLY + s)
+            if 0 <= s < CHUNKS:
+                quantise_w(s)
+            if 0 <= s - 2 < STEPS:
+                quantise(s - 2)
+            if done < STEPS and done % CHUNKS == CHUNKS - 1 and s >= 0:
+                stats_newton(done // CHUNKS)
+            for cs in stat_chunks:
+                chunk_stats(cs, second_half)
+                if cs % CHUNKS == CHUNKS - 1:
+                    stats_aggregate(cs // CHUNKS)
+            if 0 <= s < STEPS and s % CHUNKS == 4:
+                other_terms_add(s // CHUNKS)
+            if 0 <= s - 3 < STEPS:
+                multiply(s - 3)
+            if 0 <= s - 4 < STEPS and (s - 4) % CHUNKS == CHUNKS - 1:
+                store_group((s - 4) // CHUNKS)

@@ -34,11 +34,9 @@ BN_DIM = 6
 BN_PER_CHUNK = CHUNK // BN_WIDTH
 RUN = 4
 STEPS = GROUPS * CHUNKS
-STATS_LEAD = 10
+STATS_LEAD = 12
 LOAD_AHEAD = 4
 W_EARLY = 6
-VECTOR_BLOCKS_MAIN = 0
-VECTOR_BLOCKS_TAIL = 12
 
 FLOPS = 2 * ROWS * K * C_OUT
 
@@ -88,7 +86,7 @@ def tile_templatepairembeddermultimer_pa_k_kernel(
         const = pools.enter_context(tc.tile_pool(name="const", bufs=1))
         w_loads = pools.enter_context(tc.tile_pool(name="w_loads", bufs=CHUNKS))
         w_stage = pools.enter_context(tc.tile_pool(name="w_stage", bufs=CHUNKS))
-        x_pool = pools.enter_context(tc.tile_pool(name="x_pool", bufs=STATS_LEAD + LOAD_AHEAD + 2))
+        x_pool = pools.enter_context(tc.tile_pool(name="x_pool", bufs=STATS_LEAD + LOAD_AHEAD + 1))
         work = pools.enter_context(tc.tile_pool(name="work", bufs=3))
         small = pools.enter_context(tc.tile_pool(name="small", bufs=2))
         banks = pools.enter_context(tc.psum_pool(name="banks", bufs=6))
@@ -99,6 +97,7 @@ def tile_templatepairembeddermultimer_pa_k_kernel(
         make_identity(nc, ident[:])
         eps_col = const.tile([P, 1], F32, name="eps_col")
         nc.vector.memset(eps_col[:], LN_EPS)
+        seen = const.tile([P, 1], U32, name="seen")
         warm = const.tile([P, 1], F32, name="warm")
         nc.scalar.activation(out=warm[:], in_=eps_col[:], func=ACT.Abs_reciprocal_sqrt)
 
@@ -147,20 +146,21 @@ def tile_templatepairembeddermultimer_pa_k_kernel(
         vectors_b = const.tile([P, C_OUT], BF16, name="vectors_b")
         features = const.tile([P, ROWS], F32, name="features")
         dgram = const.tile([P, GROUPS, C_OUT], BF16, name="dgram")
+        nc.gpsimd.memset(features[:], 0.0)
         nc.gpsimd.memset(unit[:], 1.0)
         nc.gpsimd.memset(chain[:], 1.0)
         nc.gpsimd.memset(resid[:], 1.0)
         nc.gpsimd.memset(vectors_a[:], 0.0)
         nc.gpsimd.memset(vectors_b[:], 0.0)
         for f, vec in enumerate((unit_x, unit_y, unit_z)):
-            nc.gpsimd.dma_start(
+            nc.scalar.dma_start(
                 out=unit[f + 1 : f + 2, :], in_=vec.rearrange("i j -> (i j)").unsqueeze(0)
             )
-        nc.gpsimd.dma_start(
+        nc.scalar.dma_start(
             out=chain[0:5, :], in_=multichain_mask_2d.rearrange("i j -> (i j)").partition_broadcast(5)
         )
-        nc.gpsimd.dma_start(out=resid[0:1, :], in_=pseudo_beta_mask.unsqueeze(0))
-        nc.gpsimd.dma_start(out=resid[1:5, :], in_=backbone_mask.partition_broadcast(4))
+        nc.scalar.dma_start(out=resid[0:1, :], in_=pseudo_beta_mask.unsqueeze(0))
+        nc.scalar.dma_start(out=resid[1:5, :], in_=backbone_mask.partition_broadcast(4))
         single_rows = (
             w_pbm,
             w_x,
@@ -175,16 +175,15 @@ def tile_templatepairembeddermultimer_pa_k_kernel(
             b_bb.unsqueeze(0),
         )
         for f, vec in enumerate(single_rows):
-            nc.gpsimd.dma_start(out=vectors_a[f : f + 1, :], in_=vec)
-        nc.gpsimd.dma_start(out=vectors_a[32:64, :], in_=aa_proj1)
-        nc.gpsimd.dma_start(out=vectors_b[32:64, :], in_=esm_proj1)
-        nc.gpsimd.dma_start(out=vectors_a[64:96, :], in_=aa_proj2)
-        nc.gpsimd.dma_start(out=vectors_b[64:96, :], in_=esm_proj2)
-        nc.gpsimd.dma_start(
+            nc.scalar.dma_start(out=vectors_a[f : f + 1, :], in_=vec)
+        nc.scalar.dma_start(out=vectors_a[32:64, :], in_=aa_proj1)
+        nc.scalar.dma_start(out=vectors_b[32:64, :], in_=esm_proj1)
+        nc.scalar.dma_start(out=vectors_a[64:96, :], in_=aa_proj2)
+        nc.scalar.dma_start(out=vectors_b[64:96, :], in_=esm_proj2)
+        nc.scalar.dma_start(
             out=dgram[:], in_=act_dgram.flatten_outer_dims().rearrange("(n p) c -> p n c", p=P)
         )
         pair_shape = [N_RES, N_RES, N_RES]
-        nc.gpsimd.memset(features[:], 0.0)
         masked = features[0:N_RES, :]
         masked_ij = masked.rearrange("f (i j) -> f i j", j=N_RES)
         nc.gpsimd.tensor_tensor(out=masked, in0=unit[:], in1=chain[:], op=ALU.mult)
@@ -197,11 +196,11 @@ def tile_templatepairembeddermultimer_pa_k_kernel(
         feature_w = const.tile([P, C_OUT], F32, name="feature_w")
         nc.gpsimd.tensor_tensor(out=feature_w[:], in0=vectors_a[:], in1=vectors_b[:], op=ALU.add)
 
-        nc.gpsimd.tensor_copy(
+        nc.scalar.copy(
             out=features[32:64, :].rearrange("f (i j) -> f i j", j=N_RES),
             in_=ident[32:64, 32:64].unsqueeze(1).to_broadcast(pair_shape),
         )
-        nc.gpsimd.tensor_copy(
+        nc.scalar.copy(
             out=features[64:96, :].rearrange("f (i j) -> f i j", j=N_RES),
             in_=ident[64:96, 64:96].unsqueeze(2).to_broadcast(pair_shape),
         )
@@ -259,10 +258,7 @@ def tile_templatepairembeddermultimer_pa_k_kernel(
         def stats_aggregate(n):
             mean_var = small.tile([P, 2], F32, name="mean_var")
             nc.vector.bn_aggr(out=mean_var[:], in_=stats_of[n][:].rearrange("p b s -> p (b s)"))
-            var_eps = small.tile([P, 1], F32, name="var_eps")
-            nc.vector.tensor_scalar_add(out=var_eps[:], in0=mean_var[:, 1:2], scalar1=LN_EPS)
             mean_var_of[n] = mean_var
-            var_eps_of[n] = var_eps
 
         def stats_table(n):
             rough = small.tile([P, 1], F32, name="rough")
@@ -277,6 +273,9 @@ def tile_templatepairembeddermultimer_pa_k_kernel(
 
         def stats_newton(n):
             rough = rough_of[n]
+            var_eps = small.tile([P, 1], F32, name="var_eps")
+            nc.vector.tensor_scalar_add(out=var_eps[:], in0=mean_var_of[n][:, 1:2], scalar1=LN_EPS)
+            var_eps_of[n] = var_eps
             ratio = small.tile([P, 1], F32, name="ratio")
             nc.vector.scalar_tensor_tensor(
                 out=ratio[:], in0=var_eps_of[n][:], scalar=rough[:], in1=rough[:], op0=ALU.mult, op1=ALU.mult
@@ -301,29 +300,26 @@ def tile_templatepairembeddermultimer_pa_k_kernel(
         product_of = {}
         others_of = {}
 
-        def normalise(s):
+        def normalise(s, on_scalar):
             mean, rstd, offset = scalars_of[s // CHUNKS]
             x_hat = work.tile([P, CHUNK], F32, name="x_hat")
-            has_stats = s - 1 + STATS_LEAD < STEPS
-            split = CHUNK - P * (VECTOR_BLOCKS_MAIN if has_stats else VECTOR_BLOCKS_TAIL)
-            if split > 0:
+            if on_scalar:
                 nc.scalar.activation(
-                    out=x_hat[:, 0:split],
-                    in_=x_chunks[s][:, 0:split],
-                    func=ACT.Identity,
-                    scale=rstd[:],
-                    bias=offset[:],
+                    out=x_hat[:], in_=x_chunks[s][:], func=ACT.Identity, scale=rstd[:], bias=offset[:]
                 )
-            if split < CHUNK:
-                nc.vector.tensor_scalar(
-                    out=x_hat[:, split:CHUNK],
-                    in0=x_chunks[s][:, split:CHUNK],
-                    scalar1=mean,
-                    scalar2=rstd[:],
-                    op0=ALU.subtract,
-                    op1=ALU.mult,
+            else:
+                nc.gpsimd.tensor_scalar(
+                    out=x_hat[:],
+                    in0=x_chunks[s][:],
+                    scalar1=rstd[:],
+                    scalar2=offset[:],
+                    op0=ALU.mult,
+                    op1=ALU.add,
                 )
             x_hat_of[s] = x_hat
+
+        def wait_for_quantise(s):
+            nc.gpsimd.tensor_copy(out=seen[:], in_=codes_of[s][0][:, 0:1])
 
         def flip(s):
             banks_of[s] = []
@@ -336,25 +332,40 @@ def tile_templatepairembeddermultimer_pa_k_kernel(
                     )
                 banks_of[s].append(flipped)
 
-        def scale_shift(s):
+        def vector_banks(s):
+            if s + STATS_LEAD > STEPS:
+                return (0, 1, 2)
+            return (1,) if s % 2 == 1 else (0, 1)
+
+        def new_planes(s):
+            planes_of[s] = work.tile([P, PACK, CHUNK_WORDS], BF16, name="planes")
+
+        def scale_shift(s, a):
             c = s % CHUNKS
-            planes = work.tile([P, PACK, CHUNK_WORDS], BF16, name="planes")
-            for a in range(CHUNK_PASSES):
-                for t in range(PACK):
-                    b = (c * CHUNK_PASSES + a) * PACK + t
+            for t in range(PACK):
+                b = (c * CHUNK_PASSES + a) * PACK + t
+                if a in vector_banks(s):
+                    nc.vector.tensor_scalar(
+                        out=planes_of[s][:, t, a * P : (a + 1) * P],
+                        in0=banks_of[s][a][:, t, :],
+                        scalar1=gain_cols[:, b : b + 1],
+                        scalar2=shift_cols[:, b : b + 1],
+                        op0=ALU.mult,
+                        op1=ALU.add,
+                    )
+                else:
                     nc.scalar.activation(
-                        out=planes[:, t, a * P : (a + 1) * P],
+                        out=planes_of[s][:, t, a * P : (a + 1) * P],
                         in_=banks_of[s][a][:, t, :],
                         func=ACT.Identity,
                         scale=gain_cols[:, b : b + 1],
                         bias=shift_cols[:, b : b + 1],
                     )
-            planes_of[s] = planes
 
         def regroup(s):
             grouped = work.tile([P, CHUNK_WORDS, PACK], BF16, name="grouped", align_bytes=64)
             dst, src = regroup_views(grouped[:], planes_of[s][:])
-            nc.vector.tensor_copy(out=dst, in_=src)
+            nc.scalar.copy(out=dst, in_=src)
             grouped_of[s] = grouped
 
         def quantise(s):
@@ -409,45 +420,59 @@ def tile_templatepairembeddermultimer_pa_k_kernel(
         stats_table(0)
         stats_newton(0)
 
-        first_half = (0, 1)
-        second_half = (2, 3)
-        for s in range(-1, STEPS + 4):
-            ahead = s + STATS_LEAD + LOAD_AHEAD
+        all_pieces = (0, 1, 2, 3)
+        stats_next = CHUNKS
+        aggregated = []
+        normalise(0, True)
+        normalise(1, False)
+        flip(0)
+        for s in range(0, STEPS + 4):
+            ahead = s + STATS_LEAD + LOAD_AHEAD - 1
             if ahead < STEPS:
                 load_x(ahead)
-            stat_chunks = tuple(range(CHUNKS, STATS_LEAD)) if s == -1 else (s + STATS_LEAD,)
-            if stat_chunks[0] >= STEPS:
-                stat_chunks = ()
-            if 0 <= s + 1 < STEPS:
-                normalise(s + 1)
-            if 0 <= s < STEPS:
-                flip(s)
-                if s % CHUNKS == 4:
-                    other_terms_matmul(s // CHUNKS)
+            live = s < STEPS
+            if s + 1 < STEPS:
+                flip(s + 1)
+            if live and s % CHUNKS == 4:
+                other_terms_matmul(s // CHUNKS)
+            if 0 <= s - 3 < STEPS:
+                multiply(s - 3)
+            if live:
+                new_planes(s)
+                for a in vector_banks(s):
+                    scale_shift(s, a)
+                if 0 not in vector_banks(s):
+                    scale_shift(s, 0)
+            fresh = aggregated
+            aggregated = []
+            for n in fresh:
+                stats_table(n)
             if 0 <= s - 1 < STEPS:
                 regroup(s - 1)
-            for cs in stat_chunks:
-                chunk_stats(cs, first_half)
-            done = s - 1 + STATS_LEAD
-            if done < STEPS and done % CHUNKS == CHUNKS - 1 and s >= 0:
-                stats_table(done // CHUNKS)
-            if 0 <= s < STEPS:
-                scale_shift(s)
-            if 0 <= s < CHUNKS - W_EARLY:
+            if live:
+                for a in (2, 3):
+                    if a not in vector_banks(s):
+                        scale_shift(s, a)
+            if s < CHUNKS - W_EARLY:
                 regroup_w(W_EARLY + s)
-            if 0 <= s < CHUNKS:
+            for n in fresh:
+                stats_newton(n)
+            if s < CHUNKS:
                 quantise_w(s)
             if 0 <= s - 2 < STEPS:
                 quantise(s - 2)
-            if done < STEPS and done % CHUNKS == CHUNKS - 1 and s >= 0:
-                stats_newton(done // CHUNKS)
-            for cs in stat_chunks:
-                chunk_stats(cs, second_half)
-                if cs % CHUNKS == CHUNKS - 1:
-                    stats_aggregate(cs // CHUNKS)
-            if 0 <= s < STEPS and s % CHUNKS == 4:
+                if s + 2 < STEPS:
+                    wait_for_quantise(s - 2)
+            if s + 2 < STEPS:
+                normalise(s + 2, False)
+            for turn in range(2):
+                if stats_next < min(STEPS, s + STATS_LEAD):
+                    chunk_stats(stats_next, all_pieces)
+                    if stats_next % CHUNKS == CHUNKS - 1:
+                        stats_aggregate(stats_next // CHUNKS)
+                        aggregated.append(stats_next // CHUNKS)
+                    stats_next += 1
+            if live and s % CHUNKS == 4:
                 other_terms_add(s // CHUNKS)
-            if 0 <= s - 3 < STEPS:
-                multiply(s - 3)
             if 0 <= s - 4 < STEPS and (s - 4) % CHUNKS == CHUNKS - 1:
                 store_group((s - 4) // CHUNKS)

from contextlib import ExitStack

import concourse.mybir as mybir
from concourse.masks import make_identity

F32 = mybir.dt.float32
BF16 = mybir.dt.bfloat16
U32 = mybir.dt.uint32
U8 = mybir.dt.uint8
FP8X4 = mybir.dt.float8_e4m3fn_x4
ALU = mybir.AluOpType
ACT = mybir.ActivationFunctionType

P = 128
N_RES = 32
ROWS = N_RES * N_RES
K = 16384
C_OUT = 128
LN_EPS = 1e-5

PACK = 4
K_PASS = P * PACK
PASSES = K // K_PASS
GROUPS = ROWS // P
CHUNK_PASSES = 4
CHUNK = CHUNK_PASSES * K_PASS
CHUNKS = K // CHUNK
CHUNK_WORDS = CHUNK // PACK
CHUNK_BLOCKS = CHUNK // P
K_BLOCKS = K // P

BN_WIDTH = 512
BN_DIM = 6
BN_PER_CHUNK = CHUNK // BN_WIDTH
RUN = 4
STEPS = GROUPS * CHUNKS
STATS_LEAD = 12
LOAD_AHEAD = 4
W_EARLY = 6

FLOPS = 2 * ROWS * K * C_OUT


def regroup_views(grouped, planes):
    dst = grouped.rearrange("p (w i) t -> p w t i", i=RUN)
    src = planes.rearrange("p t (w i) -> p w t i", i=RUN)
    return dst, src


def tile_templatepairembeddermultimer_pa_k_kernel(
    tc,
    act_dgram,
    aa_proj1,
    aa_proj2,
    esm_proj1,
    esm_proj2,
    query_embedding,
    pseudo_beta_mask,
    backbone_mask,
    multichain_mask_2d,
    unit_x,
    unit_y,
    unit_z,
    ln_g,
    ln_b,
    w_q,
    b_q,
    w_pbm,
    b_pbm,
    w_x,
    b_x,
    w_y,
    b_y,
    w_z,
    b_z,
    w_bb,
    b_bb,
    out,
):
    nc = tc.nc
    x_rows = query_embedding.flatten_outer_dims()
    out_rows = out.flatten_outer_dims()


    with ExitStack() as pools:
        const = pools.enter_context(tc.tile_pool(name="const", bufs=1))
        w_loads = pools.enter_context(tc.tile_pool(name="w_loads", bufs=CHUNKS))
        w_stage = pools.enter_context(tc.tile_pool(name="w_stage", bufs=CHUNKS))
        x_pool = pools.enter_context(tc.tile_pool(name="x_pool", bufs=STATS_LEAD + LOAD_AHEAD + 1))
        work = pools.enter_context(tc.tile_pool(name="work", bufs=3))
        small = pools.enter_context(tc.tile_pool(name="small", bufs=2))
        banks = pools.enter_context(tc.psum_pool(name="banks", bufs=6))
        sums = pools.enter_context(tc.psum_pool(name="sums", bufs=2))
        pools.enter_context(tc.manual_schedule())

        ident = const.tile([P, P], F32, name="ident")
        make_identity(nc, ident[:])
        eps_col = const.tile([P, 1], F32, name="eps_col")
        nc.vector.memset(eps_col[:], LN_EPS)
        seen = const.tile([P, 1], U32, name="seen")
        warm = const.tile([P, 1], F32, name="warm")
        nc.scalar.activation(out=warm[:], in_=eps_col[:], func=ACT.Abs_reciprocal_sqrt)

        gain_rows = const.tile([P, P], BF16, name="gain_rows")
        shift_rows = const.tile([P, P], BF16, name="shift_rows")
        nc.sync.dma_start(out=gain_rows[:], in_=ln_g.rearrange("(b p) -> b p", p=P))
        nc.sync.dma_start(out=shift_rows[:], in_=ln_b.rearrange("(b p) -> b p", p=P))

        x_chunks = {}
        w_raws = {}
        w_blocks = w_q.rearrange("(b p) n -> p b n", p=P)

        def load_x(s):
            n, c = divmod(s, CHUNKS)
            x_chunk = x_pool.tile([P, CHUNK], BF16, name="x_chunk")
            nc.sync.dma_start(
                out=x_chunk[:], in_=x_rows[n * P : (n + 1) * P, c * CHUNK : (c + 1) * CHUNK]
            )
            x_chunks[s] = x_chunk

        def load_w(c):
            w_raw = w_loads.tile([P, CHUNK_PASSES * PACK, C_OUT], BF16, name="w_raw")
            first = c * CHUNK_PASSES * PACK
            nc.sync.dma_start(out=w_raw[:], in_=w_blocks[:, first : first + CHUNK_PASSES * PACK, :])
            w_raws[c] = w_raw

        x_chunks[0] = x_pool.tile([P, CHUNK], BF16, name="x_chunk")
        w_raws[0] = w_loads.tile([P, CHUNK_PASSES * PACK, C_OUT], BF16, name="w_raw")
        for a in range(CHUNK_PASSES):
            nc.sync.dma_start(
                out=x_chunks[0][:, a * K_PASS : (a + 1) * K_PASS], in_=x_rows[0:P, a * K_PASS : (a + 1) * K_PASS]
            )
            nc.sync.dma_start(
                out=w_raws[0][:, a * PACK : (a + 1) * PACK, :], in_=w_blocks[:, a * PACK : (a + 1) * PACK, :]
            )
        for s in range(1, CHUNKS):
            load_x(s)
            load_w(s)
        for s in range(CHUNKS, STATS_LEAD + LOAD_AHEAD - 1):
            load_x(s)

        unit = const.tile([N_RES, ROWS], BF16, name="unit")
        chain = const.tile([N_RES, ROWS], BF16, name="chain")
        resid = const.tile([N_RES, N_RES], BF16, name="resid")
        vectors_a = const.tile([P, C_OUT], BF16, name="vectors_a")
        vectors_b = const.tile([P, C_OUT], BF16, name="vectors_b")
        features = const.tile([P, ROWS], F32, name="features")
        dgram = const.tile([P, GROUPS, C_OUT], BF16, name="dgram")
        nc.gpsimd.memset(features[:], 0.0)
        nc.gpsimd.memset(unit[:], 1.0)
        nc.gpsimd.memset(chain[:], 1.0)
        nc.gpsimd.memset(resid[:], 1.0)
        nc.gpsimd.memset(vectors_a[:], 0.0)
        nc.gpsimd.memset(vectors_b[:], 0.0)
        for f, vec in enumerate((unit_x, unit_y, unit_z)):
            nc.scalar.dma_start(
                out=unit[f + 1 : f + 2, :], in_=vec.rearrange("i j -> (i j)").unsqueeze(0)
            )
        nc.scalar.dma_start(
            out=chain[0:5, :], in_=multichain_mask_2d.rearrange("i j -> (i j)").partition_broadcast(5)
        )
        nc.scalar.dma_start(out=resid[0:1, :], in_=pseudo_beta_mask.unsqueeze(0))
        nc.scalar.dma_start(out=resid[1:5, :], in_=backbone_mask.partition_broadcast(4))
        single_rows = (
            w_pbm,
            w_x,
            w_y,
            w_z,
            w_bb,
            b_q.unsqueeze(0),
            b_pbm.unsqueeze(0),
            b_x.unsqueeze(0),
            b_y.unsqueeze(0),
            b_z.unsqueeze(0),
            b_bb.unsqueeze(0),
        )
        for f, vec in enumerate(single_rows):
            nc.scalar.dma_start(out=vectors_a[f : f + 1, :], in_=vec)
        nc.scalar.dma_start(out=vectors_a[32:64, :], in_=aa_proj1)
        nc.scalar.dma_start(out=vectors_b[32:64, :], in_=esm_proj1)
        nc.scalar.dma_start(out=vectors_a[64:96, :], in_=aa_proj2)
        nc.scalar.dma_start(out=vectors_b[64:96, :], in_=esm_proj2)
        nc.scalar.dma_start(
            out=dgram[:], in_=act_dgram.flatten_outer_dims().rearrange("(n p) c -> p n c", p=P)
        )
        pair_shape = [N_RES, N_RES, N_RES]
        masked = features[0:N_RES, :]
        masked_ij = masked.rearrange("f (i j) -> f i j", j=N_RES)
        nc.gpsimd.tensor_tensor(out=masked, in0=unit[:], in1=chain[:], op=ALU.mult)
        nc.gpsimd.tensor_tensor(
            out=masked_ij, in0=masked_ij, in1=resid[:].unsqueeze(2).to_broadcast(pair_shape), op=ALU.mult
        )
        nc.gpsimd.tensor_tensor(
            out=masked_ij, in0=masked_ij, in1=resid[:].unsqueeze(1).to_broadcast(pair_shape), op=ALU.mult
        )
        feature_w = const.tile([P, C_OUT], F32, name="feature_w")
        nc.gpsimd.tensor_tensor(out=feature_w[:], in0=vectors_a[:], in1=vectors_b[:], op=ALU.add)

        nc.scalar.copy(
            out=features[32:64, :].rearrange("f (i j) -> f i j", j=N_RES),
            in_=ident[32:64, 32:64].unsqueeze(1).to_broadcast(pair_shape),
        )
        nc.scalar.copy(
            out=features[64:96, :].rearrange("f (i j) -> f i j", j=N_RES),
            in_=ident[64:96, 64:96].unsqueeze(2).to_broadcast(pair_shape),
        )

        def k_block_columns(rows_bf16, name):
            rows_f32 = const.tile([P, P], F32, name=name + "_rows_f32")
            nc.vector.tensor_copy(out=rows_f32[:], in_=rows_bf16[:])
            flipped = banks.tile([P, P], F32, name=name + "_flipped", tag="bank")
            nc.tensor.transpose(out=flipped[:], in_=rows_f32[:], identity=ident[:])
            cols = const.tile([P, K_BLOCKS], F32, name=name + "_cols")
            nc.vector.tensor_copy(out=cols[:], in_=flipped[:])
            return cols

        gain_cols = k_block_columns(gain_rows, "gain")
        shift_cols = k_block_columns(shift_rows, "shift")

        w_codes = const.tile([P, PASSES * C_OUT], U32, name="w_codes", align_bytes=64)
        w_scales = const.tile([P, PASSES * C_OUT], U8, name="w_scales", align_bytes=64)
        w_grouped_of = {}

        def regroup_w(c):
            w_grouped = w_stage.tile([P, CHUNK_WORDS, PACK], BF16, name="w_grouped", align_bytes=64)
            for a in range(CHUNK_PASSES):
                dst, src = regroup_views(
                    w_grouped[:, a * C_OUT : (a + 1) * C_OUT, :],
                    w_raws[c][:, a * PACK : (a + 1) * PACK, :],
                )
                nc.scalar.copy(out=dst, in_=src)
            w_grouped_of[c] = w_grouped

        def quantise_w(c):
            words = slice(c * CHUNK_WORDS, (c + 1) * CHUNK_WORDS)
            nc.vector.quantize_mx(
                out=w_codes[:, words].bitcast(FP8X4),
                scales=w_scales[:, words],
                in_=w_grouped_of[c][:].rearrange("p w t -> p (w t)"),
            )

        stats_of = {}
        mean_var_of = {}
        rough_of = {}
        var_eps_of = {}
        scalars_of = {}

        def chunk_stats(s, pieces):
            n, c = divmod(s, CHUNKS)
            if c == 0 and pieces[0] == 0:
                stats_of[n] = small.tile([P, K // BN_WIDTH, BN_DIM], F32, name="stats")
            for piece in pieces:
                nc.vector.bn_stats(
                    out=stats_of[n][:, c * BN_PER_CHUNK + piece, :],
                    in_=x_chunks[s][:, piece * BN_WIDTH : (piece + 1) * BN_WIDTH],
                )

        def stats_aggregate(n):
            mean_var = small.tile([P, 2], F32, name="mean_var")
            nc.vector.bn_aggr(out=mean_var[:], in_=stats_of[n][:].rearrange("p b s -> p (b s)"))
            mean_var_of[n] = mean_var

        def stats_table(n):
            rough = small.tile([P, 1], F32, name="rough")
            nc.scalar.activation(
                out=rough[:],
                in_=mean_var_of[n][:, 1:2],
                func=ACT.Abs_reciprocal_sqrt,
                bias=eps_col[:],
                scale=1.0,
            )
            rough_of[n] = rough

        def stats_newton(n):
            rough = rough_of[n]
            var_eps = small.tile([P, 1], F32, name="var_eps")
            nc.vector.tensor_scalar_add(out=var_eps[:], in0=mean_var_of[n][:, 1:2], scalar1=LN_EPS)
            var_eps_of[n] = var_eps
            ratio = small.tile([P, 1], F32, name="ratio")
            nc.vector.scalar_tensor_tensor(
                out=ratio[:], in0=var_eps_of[n][:], scalar=rough[:], in1=rough[:], op0=ALU.mult, op1=ALU.mult
            )
            newton = small.tile([P, 1], F32, name="newton")
            nc.vector.tensor_scalar(
                out=newton[:], in0=ratio[:], scalar1=-0.5, scalar2=1.5, op0=ALU.mult, op1=ALU.add
            )
            rstd = small.tile([P, 1], F32, name="rstd")
            nc.vector.tensor_mul(out=rstd[:], in0=rough[:], in1=newton[:])
            offset = small.tile([P, 1], F32, name="offset")
            nc.vector.scalar_tensor_tensor(
                out=offset[:], in0=mean_var_of[n][:, 0:1], scalar=-1.0, in1=rstd[:], op0=ALU.mult, op1=ALU.mult
            )
            scalars_of[n] = (mean_var_of[n][:, 0:1], rstd, offset)

        x_hat_of = {}
        banks_of = {}
        planes_of = {}
        grouped_of = {}
        codes_of = {}
        product_of = {}
        others_of = {}

        def normalise(s, on_scalar):
            mean, rstd, offset = scalars_of[s // CHUNKS]
            x_hat = work.tile([P, CHUNK], F32, name="x_hat")
            if on_scalar:
                nc.scalar.activation(
                    out=x_hat[:], in_=x_chunks[s][:], func=ACT.Identity, scale=rstd[:], bias=offset[:]
                )
            else:
                nc.gpsimd.tensor_scalar(
                    out=x_hat[:],
                    in0=x_chunks[s][:],
                    scalar1=rstd[:],
                    scalar2=offset[:],
                    op0=ALU.mult,
                    op1=ALU.add,
                )
            x_hat_of[s] = x_hat

        def wait_for_quantise(s):
            nc.gpsimd.tensor_copy(out=seen[:], in_=codes_of[s][0][:, 0:1])

        def flip(s):
            banks_of[s] = []
            for a in range(CHUNK_PASSES):
                flipped = banks.tile([P, PACK, P], F32, name="flipped", tag="bank")
                for t in range(PACK):
                    b = a * PACK + t
                    nc.tensor.transpose(
                        out=flipped[:, t, :], in_=x_hat_of[s][:, b * P : (b + 1) * P], identity=ident[:]
                    )
                banks_of[s].append(flipped)

        def vector_banks(s):
            if s + STATS_LEAD > STEPS:
                return (0, 1, 2)
            return (1,) if s % 2 == 1 else (0, 1)

        def new_planes(s):
            planes_of[s] = work.tile([P, PACK, CHUNK_WORDS], BF16, name="planes")

        def scale_shift(s, a):
            c = s % CHUNKS
            for t in range(PACK):
                b = (c * CHUNK_PASSES + a) * PACK + t
                if a in vector_banks(s):
                    nc.vector.tensor_scalar(
                        out=planes_of[s][:, t, a * P : (a + 1) * P],
                        in0=banks_of[s][a][:, t, :],
                        scalar1=gain_cols[:, b : b + 1],
                        scalar2=shift_cols[:, b : b + 1],
                        op0=ALU.mult,
                        op1=ALU.add,
                    )
                else:
                    nc.scalar.activation(
                        out=planes_of[s][:, t, a * P : (a + 1) * P],
                        in_=banks_of[s][a][:, t, :],
                        func=ACT.Identity,
                        scale=gain_cols[:, b : b + 1],
                        bias=shift_cols[:, b : b + 1],
                    )

        def regroup(s):
            grouped = work.tile([P, CHUNK_WORDS, PACK], BF16, name="grouped", align_bytes=64)
            dst, src = regroup_views(grouped[:], planes_of[s][:])
            nc.scalar.copy(out=dst, in_=src)
            grouped_of[s] = grouped

        def quantise(s):
            q_codes = work.tile([P, CHUNK_WORDS], U32, name="q_codes", align_bytes=64)
            q_scales = work.tile([P, CHUNK_WORDS], U8, name="q_scales", align_bytes=64)
            nc.vector.quantize_mx(
                out=q_codes[:].bitcast(FP8X4),
                scales=q_scales[:],
                in_=grouped_of[s][:].rearrange("p w t -> p (w t)"),
            )
            codes_of[s] = (q_codes, q_scales)

        def multiply(s):
            n, c = divmod(s, CHUNKS)
            q_codes, q_scales = codes_of[s]
            if c == 0:
                product_of[n] = sums.tile([P, C_OUT], F32, name="product")
            for a in range(CHUNK_PASSES):
                g = c * CHUNK_PASSES + a
                nc.tensor.matmul_mx(
                    out=product_of[n][:],
                    lhsT=q_codes[:, a * P : (a + 1) * P].bitcast(FP8X4),
                    lhsT_scale=q_scales[:, a * P : (a + 1) * P],
                    rhs=w_codes[:, g * C_OUT : (g + 1) * C_OUT].bitcast(FP8X4),
                    rhs_scale=w_scales[:, g * C_OUT : (g + 1) * C_OUT],
                    start=(g == 0),
                    stop=(g == PASSES - 1),
                )

        def other_terms_matmul(n):
            extra = banks.tile([P, C_OUT], F32, name="extra", tag="bank")
            nc.tensor.matmul(
                out=extra[:], lhsT=features[:, n * P : (n + 1) * P], rhs=feature_w[:], start=True, stop=True
            )
            others_of[n] = extra

        def other_terms_add(n):
            others = small.tile([P, C_OUT], F32, name="others")
            nc.vector.tensor_tensor(out=others[:], in0=others_of[n][:], in1=dgram[:, n, :], op=ALU.add)
            others_of[n] = others

        def store_group(n):
            result = small.tile([P, C_OUT], F32, name="result")
            nc.vector.tensor_tensor(out=result[:], in0=product_of[n][:], in1=others_of[n][:], op=ALU.add)
            nc.sync.dma_start(out=out_rows[n * P : (n + 1) * P, :], in_=result[:])

        for c in range(W_EARLY):
            regroup_w(c)
        for s in range(CHUNKS):
            chunk_stats(s, (0, 1, 2, 3))
        stats_aggregate(0)
        stats_table(0)
        stats_newton(0)

        all_pieces = (0, 1, 2, 3)
        stats_next = CHUNKS
        aggregated = []
        normalise(0, True)
        normalise(1, False)
        flip(0)
        for s in range(0, STEPS + 4):
            ahead = s + STATS_LEAD + LOAD_AHEAD - 1
            if ahead < STEPS:
                load_x(ahead)
            live = s < STEPS
            if s + 1 < STEPS:
                flip(s + 1)
            if live and s % CHUNKS == 4:
                other_terms_matmul(s // CHUNKS)
            if 0 <= s - 3 < STEPS:
                multiply(s - 3)
            if live:
                new_planes(s)
                for a in vector_banks(s):
                    scale_shift(s, a)
                if 0 not in vector_banks(s):
                    scale_shift(s, 0)
            fresh = aggregated
            aggregated = []
            for n in fresh:
                stats_table(n)
            if 0 <= s - 1 < STEPS:
                regroup(s - 1)
            if live:
                for a in (2, 3):
                    if a not in vector_banks(s):
                        scale_shift(s, a)
            if s < CHUNKS - W_EARLY:
                regroup_w(W_EARLY + s)
            for n in fresh:
                stats_newton(n)
            if s < CHUNKS:
                quantise_w(s)
            if 0 <= s - 2 < STEPS:
                quantise(s - 2)
                if s + 2 < STEPS:
                    wait_for_quantise(s - 2)
            if s + 2 < STEPS:
                normalise(s + 2, False)
            for turn in range(2):
                if stats_next < min(STEPS, s + STATS_LEAD):
                    chunk_stats(stats_next, all_pieces)
                    if stats_next % CHUNKS == CHUNKS - 1:
                        stats_aggregate(stats_next // CHUNKS)
                        aggregated.append(stats_next // CHUNKS)
                    stats_next += 1
            if live and s % CHUNKS == 4:
                other_terms_add(s // CHUNKS)
            if 0 <= s - 4 < STEPS and (s - 4) % CHUNKS == CHUNKS - 1:
                store_group((s - 4) // CHUNKS)
